import numpy as np
import ml_dtypes


def mxq(x, axis, fmt="e4m3"):
    dtype, down = {"e4m3": (ml_dtypes.float8_e4m3fn, 7), "e5m2": (ml_dtypes.float8_e5m2, 14)}[fmt]
    v = np.moveaxis(np.asarray(x, np.float32).astype(ml_dtypes.bfloat16).astype(np.float64), axis, -1)
    blocks = v.reshape(v.shape[:-1] + (-1, 32))
    amax = np.abs(blocks).max(-1, keepdims=True)
    byte = np.maximum(np.where(amax > 0, np.frexp(amax)[1] - 1 + 127, 0) - down, 1)
    scale = np.exp2(byte - 127.0)
    codes = (blocks / scale).astype(np.float32).astype(dtype).astype(np.float64)
    return np.moveaxis((codes * scale).reshape(v.shape), -1, axis)


WIDE = False


def mx_kscale(k):
    if not WIDE:
        return np.ones(k)
    levels = np.array([10, -10, 5, -5, 0])
    a = np.random.permutation(np.resize(levels, k // 512 * 4)).reshape(k // 512, 4)
    idx = np.arange(k)
    return np.exp2(a[idx // 512, idx % 128 // 32])


BF16 = ml_dtypes.bfloat16


def bf(x):
    return np.asarray(x, np.float32).astype(BF16)


def f64(x):
    return np.asarray(x).astype(np.float64)


E2M1 = np.array([0.0, 0.5, 1.0, 1.5, 2.0, 3.0, 4.0, 6.0, -0.0, -0.5, -1.0, -1.5, -2.0, -3.0, -4.0, -6.0])


def pack_weight(w, fmt):
    k, n = w.shape
    w = f64(bf(w)).reshape(k // 32, 32, n)
    amax = np.abs(w).max(1)
    if fmt == "e4m3":
        byte = np.frexp(amax)[1] - 1 + 127 - 7
    else:
        mant, ex = np.frexp(amax / 6.0)
        byte = np.where(mant > 0.5, ex, ex - 1) + 127
    byte = np.clip(np.where(amax > 0, byte, 1), 1, 254)
    scaled = (w * np.exp2(127.0 - byte)[:, None, :]).reshape(k, n).astype(np.float32)
    by_word = np.ascontiguousarray(scaled.reshape(k // 512, 128, 4, n).transpose(0, 1, 3, 2))
    if fmt == "e4m3":
        words = by_word.astype(ml_dtypes.float8_e4m3fn).view(np.uint8)
    else:
        c = by_word.astype(ml_dtypes.float4_e2m1fn).view(np.uint8) & 0xF
        words = c[..., 0::2] | (c[..., 1::2] << 4)
    return np.ascontiguousarray(words), np.ascontiguousarray(byte.astype(np.uint8).reshape(k // 512, 16, n))


def unpack_weight(words, scales, fmt):
    g, p, n, _ = words.shape
    if fmt == "e4m3":
        vals = np.ascontiguousarray(words).view(ml_dtypes.float8_e4m3fn).astype(np.float64)
    else:
        nib = np.empty((g, p, n, 4), np.uint8)
        nib[..., 0::2] = words & 0xF
        nib[..., 1::2] = words >> 4
        vals = E2M1[nib]
    vals = vals * np.repeat(np.exp2(scales.astype(np.float64) - 127.0), 8, axis=1)[..., None]
    return vals.transpose(0, 1, 3, 2).reshape(g * 512, n)


B, N, E, H, NOPE, VDIM, ROPE, QR, KVR = 4, 1024, 1024, 4, 64, 64, 128, 512, 512
KVH = NOPE + VDIM
BASE = 10000.0
FMT = "e4m3"


def rope(v):
    d = v.shape[-1]
    n = v.shape[-2]
    theta = BASE ** (-2.0 * np.arange(d // 2) / d)
    ang = np.arange(n)[:, None] * theta[None, :]
    cos, sin = np.cos(ang), np.sin(ang)
    v1, v2 = v[..., 0::2], v[..., 1::2]
    return np.stack([v1 * cos - v2 * sin, v1 * sin + v2 * cos], axis=-1).reshape(v.shape)


def setup_inputs():
    s, t = mx_kscale(E), mx_kscale(KVR)
    tcol = np.concatenate([t, np.ones(ROPE)])
    x = bf(np.random.standard_normal((B, N, E)) * s)
    Wkva_words, Wkva_scales = pack_weight(np.random.standard_normal((E, KVR + ROPE)) / np.sqrt(E) / s[:, None] * tcol, FMT)
    Wkvb_words, Wkvb_scales = pack_weight(np.random.standard_normal((KVR, H * KVH)) / np.sqrt(KVR) / t[:, None], FMT)
    return {"x": x,
            "Wkva_words": Wkva_words, "Wkva_scales": Wkva_scales,
            "Wkvb_words": Wkvb_words, "Wkvb_scales": Wkvb_scales}


def reference(x, Wkva_words, Wkva_scales, Wkvb_words, Wkvb_scales):
    ckv = mxq(f64(x), 2, "e4m3") @ unpack_weight(Wkva_words, Wkva_scales, FMT)
    compressed, k_pe = ckv[..., :KVR], ckv[..., KVR:]
    k_pe = np.broadcast_to(k_pe[:, None], (B, H, N, ROPE))
    kv = mxq(compressed, 2, "e4m3") @ unpack_weight(Wkvb_words, Wkvb_scales, FMT)
    kv = kv.reshape(B, N, H, KVH).transpose(0, 2, 1, 3)
    k_nope, v = kv[..., :NOPE], kv[..., NOPE:]
    kf = np.concatenate([k_nope, rope(k_pe)], axis=-1)
    return kf, v

@@ -1,0 +1,283 @@
+import math
+
+import concourse.mybir as mybir
+from concourse.masks import make_identity
+
+F32 = mybir.dt.float32
+BF16 = mybir.dt.bfloat16
+I32 = mybir.dt.int32
+U32 = mybir.dt.uint32
+U8 = mybir.dt.uint8
+FP8X4 = mybir.dt.float8_e4m3fn_x4
+ALU = mybir.AluOpType
+ACT = mybir.ActivationFunctionType
+
+P = 128
+PACK = 4
+B, N, E, H = 4, 1024, 1024, 4
+NOPE, VDIM, ROPE, KVR = 64, 64, 128, 512
+KF = NOPE + ROPE
+PAIRS = ROPE // 2
+X_PASSES = E // (P * PACK)
+CKV = KVR + ROPE
+TILES = 2
+STEP = P * TILES
+STEPS = B * N // STEP
+STEPS_PER_BATCH = N // STEP
+BASE = 10000.0
+
+FLOPS = 2 * B * N * (E * CKV + KVR * H * (NOPE + VDIM))
+
+TWO_PI_HI = 6.28125
+TWO_PI_LO = 2.0 * math.pi - TWO_PI_HI
+ROUND_MAGIC = 1.5 * 2.0**23
+
+
+def tile_multilatentattention_pb_t_kernel(
+    tc, x, Wkva_words, Wkva_scales, Wkvb_words, Wkvb_scales, kf, v
+):
+    nc = tc.nc
+    with (
+        tc.tile_pool(name="const", bufs=1) as const,
+        tc.tile_pool(name="work", bufs=2) as work,
+        tc.tile_pool(name="result", bufs=5) as result,
+        tc.psum_pool(name="psum", bufs=1) as psum,
+        tc.manual_schedule(),
+    ):
+        x_all = const.tile([P, STEPS, TILES, E], BF16)
+        x_rows = x.flatten_outer_dims().rearrange("(s p j) e -> p s j e", p=P, j=TILES)
+        wa_words = const.tile([P, X_PASSES, CKV * PACK], U8, align_bytes=64)
+        wa_scales = const.tile([P, X_PASSES, CKV], U8, align_bytes=64)
+        wb_words = const.tile([P, KVR * PACK], U8, align_bytes=64)
+        wb_scales = const.tile([P, KVR], U8, align_bytes=64)
+
+        nc.vector.memset(wa_scales[:].rearrange("p g n -> p (g n)").bitcast(I32), 0)
+        nc.vector.memset(wb_scales[:].bitcast(I32), 0)
+
+        def load_x(s):
+            nc.sync.dma_start(out=x_all[:, s], in_=x_rows[:, s])
+
+        load_x(0)
+        for quad in range(4):
+            nc.sync.dma_start(
+                out=wa_scales[32 * quad : 32 * quad + 4].bitcast(I32),
+                in_=Wkva_scales[:, 4 * quad : 4 * quad + 4, :].rearrange("g r n -> r g n").bitcast(I32),
+            )
+        nc.sync.dma_start(
+            out=wa_words[:].bitcast(I32),
+            in_=Wkva_words.rearrange("g p n t -> p g (n t)").bitcast(I32),
+        )
+        load_x(1)
+        for quad in range(4):
+            nc.sync.dma_start(
+                out=wb_scales[32 * quad : 32 * quad + 4].bitcast(I32),
+                in_=Wkvb_scales[0, 4 * quad : 4 * quad + 4, :].bitcast(I32),
+            )
+        nc.sync.dma_start(
+            out=wb_words[:].bitcast(I32),
+            in_=Wkvb_words[0].rearrange("p n t -> p (n t)").bitcast(I32),
+        )
+        for s in range(2, STEPS):
+            load_x(s)
+
+        identity = const.tile([P, P], F32)
+        make_identity(nc, identity[:])
+
+        TABLE = STEPS_PER_BATCH * TILES * PAIRS
+        position_int = const.tile([P, STEPS_PER_BATCH * TILES], I32)
+        nc.gpsimd.iota(
+            position_int[:], pattern=[[STEP, STEPS_PER_BATCH], [1, TILES]], base=0, channel_multiplier=TILES
+        )
+        position = const.tile([P, STEPS_PER_BATCH * TILES], F32)
+        nc.vector.tensor_copy(out=position[:], in_=position_int[:])
+
+        ratio = BASE ** (-2.0 / ROPE)
+        theta = const.tile([P, PAIRS], F32)
+        nc.vector.memset(theta[:, 0:1], 1.0)
+        width = 1
+        while width < PAIRS:
+            nc.vector.tensor_scalar_mul(theta[:, width : 2 * width], theta[:, 0:width], ratio**width)
+            width *= 2
+
+        angle = const.tile([P, TABLE], F32)
+        nc.vector.tensor_tensor(
+            out=angle[:].rearrange("p (n i) -> p n i", i=PAIRS),
+            in0=position[:].unsqueeze(2).to_broadcast([P, STEPS_PER_BATCH * TILES, PAIRS]),
+            in1=theta[:].unsqueeze(1).to_broadcast([P, STEPS_PER_BATCH * TILES, PAIRS]),
+            op=ALU.mult,
+        )
+        turns = const.tile([P, TABLE], F32)
+        nc.vector.tensor_scalar(
+            out=turns[:], in0=angle[:], scalar1=0.5 / math.pi, scalar2=ROUND_MAGIC, op0=ALU.mult, op1=ALU.add
+        )
+        whole_turns = const.tile([P, TABLE], F32)
+        nc.vector.tensor_scalar_add(whole_turns[:], turns[:], -ROUND_MAGIC)
+        partly_reduced = const.tile([P, TABLE], F32)
+        nc.vector.scalar_tensor_tensor(
+            out=partly_reduced[:], in0=whole_turns[:], scalar=-TWO_PI_HI, in1=angle[:], op0=ALU.mult, op1=ALU.add
+        )
+        reduced = const.tile([P, TABLE], F32)
+        nc.vector.scalar_tensor_tensor(
+            out=reduced[:], in0=whole_turns[:], scalar=-TWO_PI_LO, in1=partly_reduced[:], op0=ALU.mult, op1=ALU.add
+        )
+        sin_half = const.tile([P, TABLE], F32)
+        nc.scalar.activation(out=sin_half[:], in_=reduced[:], func=ACT.Sin, scale=0.5)
+        minus_abs = const.tile([P, TABLE], F32)
+        nc.vector.scalar_tensor_tensor(
+            out=minus_abs[:], in0=reduced[:], scalar=-1.0, in1=reduced[:], op0=ALU.mult, op1=ALU.min
+        )
+        cos_arg = const.tile([P, TABLE], F32)
+        nc.vector.tensor_scalar(
+            out=cos_arg[:], in0=minus_abs[:], scalar1=0.5, scalar2=0.5 * math.pi, op0=ALU.mult, op1=ALU.add
+        )
+        cos_half = const.tile([P, TABLE], F32)
+        nc.scalar.activation(out=cos_half[:], in_=cos_arg[:], func=ACT.Sin)
+        minus_two_sq = const.tile([P, TABLE], F32)
+        nc.vector.scalar_tensor_tensor(
+            out=minus_two_sq[:], in0=sin_half[:], scalar=-2.0, in1=sin_half[:], op0=ALU.mult, op1=ALU.mult
+        )
+        cos_table = const.tile([P, STEPS_PER_BATCH, TILES, PAIRS], F32)
+        nc.vector.tensor_scalar_add(cos_table[:].rearrange("p r j i -> p (r j i)"), minus_two_sq[:], 1.0)
+        sin_table = const.tile([P, STEPS_PER_BATCH, TILES, PAIRS], F32)
+        nc.vector.scalar_tensor_tensor(
+            out=sin_table[:].rearrange("p r j i -> p (r j i)"),
+            in0=sin_half[:], scalar=2.0, in1=cos_half[:], op0=ALU.mult, op1=ALU.mult,
+        )
+
+        x_codes, x_scales, pe_sums, c_rounded = {}, {}, {}, {}
+        c_grouped, c_codes, c_scales, kv_sums, kf_rows = {}, {}, {}, {}, {}
+
+        def quantise_x(s):
+            grouped = work.tile([P, TILES, X_PASSES, P, PACK], BF16, name="x_grouped", align_bytes=64)
+            for j in range(TILES):
+                words = x_all[:, s, j, :].bitcast(F32)
+                flipped = psum.tile([P, X_PASSES, 2, P], F32, name="x_flipped", bufs=2)
+                for g in range(X_PASSES):
+                    for u in range(2):
+                        nc.tensor.transpose(
+                            flipped[:, g, u, :], words[:, 2 * P * g + u : 2 * P * (g + 1) : 2], identity[:]
+                        )
+                nc.scalar.copy(
+                    out=grouped[:, j].bitcast(F32), in_=flipped[:].rearrange("p g u t -> p g t u")
+                )
+            x_codes[s] = work.tile([P, TILES, X_PASSES, P], U32, name="x_codes", align_bytes=64)
+            x_scales[s] = work.tile([P, TILES, X_PASSES, P], U8, name="x_scales", align_bytes=64)
+            nc.vector.quantize_mx(
+                out=x_codes[s][:].rearrange("p j g t -> p (j g t)").bitcast(FP8X4),
+                scales=x_scales[s][:].rearrange("p j g t -> p (j g t)"),
+                in_=grouped[:].rearrange("p j g t k -> p (j g t k)"),
+            )
+
+        def x_times_wkva(s, j, first, width, sums):
+            for g in range(X_PASSES):
+                nc.tensor.matmul_mx(
+                    out=sums,
+                    lhsT=x_codes[s][:, j, g, :].bitcast(FP8X4),
+                    lhsT_scale=x_scales[s][:, j, g, :],
+                    rhs=wa_words[:, g, PACK * first : PACK * (first + width)].bitcast(FP8X4),
+                    rhs_scale=wa_scales[:, g, first : first + width],
+                    start=(g == 0),
+                    stop=(g == X_PASSES - 1),
+                )
+
+        def compress(s):
+            c_rounded[s] = work.tile([P, TILES, 2, P, 2], BF16, name="c_rounded")
+            for j in range(TILES):
+                c_sums = psum.tile([P, KVR], F32, name="c_sums", bufs=2)
+                x_times_wkva(s, j, 0, KVR, c_sums[:])
+                nc.scalar.copy(
+                    out=c_rounded[s][:, j], in_=c_sums[:].rearrange("p (q u e) -> p u q e", u=2, e=2)
+                )
+            pe_sums[s] = psum.tile([P, TILES, ROPE], F32, name="pe_sums")
+            for j in range(TILES):
+                x_times_wkva(s, j, KVR, ROPE, pe_sums[s][:, j, :])
+
+        def transpose_c(s):
+            flipped = psum.tile([P, TILES, 2, P], F32, name="c_flipped")
+            for j in range(TILES):
+                for u in range(2):
+                    nc.tensor.transpose(
+                        flipped[:, j, u, :],
+                        c_rounded[s][:, j, u].rearrange("p q e -> p (q e)").bitcast(F32),
+                        identity[:],
+                    )
+            c_grouped[s] = work.tile([P, TILES, P, PACK], BF16, name="c_grouped", align_bytes=64)
+            nc.scalar.copy(
+                out=c_grouped[s][:].bitcast(F32), in_=flipped[:].rearrange("p j u t -> p j t u")
+            )
+
+        def quantise_c(s):
+            c_codes[s] = work.tile([P, TILES, P], U32, name="c_codes", align_bytes=64)
+            c_scales[s] = work.tile([P, TILES, P], U8, name="c_scales", align_bytes=64)
+            nc.vector.quantize_mx(
+                out=c_codes[s][:].rearrange("p j t -> p (j t)").bitcast(FP8X4),
+                scales=c_scales[s][:].rearrange("p j t -> p (j t)"),
+                in_=c_grouped[s][:].rearrange("p j t k -> p (j t k)"),
+            )
+
+        def rotate(s):
+            pe = pe_sums[s][:].rearrange("p j (i e) -> p j e i", e=2)
+            cos = cos_table[:, s % STEPS_PER_BATCH]
+            sin = sin_table[:, s % STEPS_PER_BATCH]
+            with_cos = work.tile([P, TILES, 2, PAIRS], F32, name="with_cos")
+            with_sin = work.tile([P, TILES, 2, PAIRS], F32, name="with_sin")
+            nc.vector.tensor_tensor(
+                out=with_cos[:], in0=pe, in1=cos.unsqueeze(2).to_broadcast([P, TILES, 2, PAIRS]), op=ALU.mult
+            )
+            nc.vector.scalar_tensor_tensor(
+                out=with_sin[:, :, 0, :], in0=pe[:, :, 1, :], scalar=-1.0, in1=sin, op0=ALU.mult, op1=ALU.mult
+            )
+            nc.vector.tensor_tensor(out=with_sin[:, :, 1, :], in0=pe[:, :, 0, :], in1=sin, op=ALU.mult)
+            kf_rows[s] = result.tile([P, H, TILES, KF], F32, name="kf_rows")
+            nc.vector.tensor_tensor(
+                out=kf_rows[s][:, 0, :, NOPE:KF].rearrange("p j (i e) -> p j i e", e=2),
+                in0=with_cos[:].rearrange("p j e i -> p j i e"),
+                in1=with_sin[:].rearrange("p j e i -> p j i e"),
+                op=ALU.add,
+            )
+            nc.vector.tensor_copy(
+                out=kf_rows[s][:, 1:H, :, NOPE:KF],
+                in_=kf_rows[s][:, 0:1, :, NOPE:KF].to_broadcast([P, H - 1, TILES, ROPE]),
+            )
+
+        def expand(s):
+            for j in range(TILES):
+                kv_sums[s, j] = psum.tile([P, H, 2, NOPE], F32, name="kv_sums", bufs=2)
+                nc.tensor.matmul_mx(
+                    out=kv_sums[s, j][:].rearrange("p h c d -> p (h c d)"),
+                    lhsT=c_codes[s][:, j, :].bitcast(FP8X4),
+                    lhsT_scale=c_scales[s][:, j, :],
+                    rhs=wb_words[:].bitcast(FP8X4),
+                    rhs_scale=wb_scales[:],
+                    start=True,
+                    stop=True,
+                )
+
+        def store(s):
+            v_rows = result.tile([P, H, TILES, VDIM], F32, name="v_rows")
+            nc.vector.tensor_copy(out=kf_rows[s][:, :, 0, 0:NOPE], in_=kv_sums[s, 0][:, :, 0, :])
+            nc.vector.tensor_copy(out=v_rows[:, :, 0, :], in_=kv_sums[s, 0][:, :, 1, :])
+            nc.scalar.copy(out=kf_rows[s][:, :, 1, 0:NOPE], in_=kv_sums[s, 1][:, :, 0, :])
+            nc.scalar.copy(out=v_rows[:, :, 1, :], in_=kv_sums[s, 1][:, :, 1, :])
+            b, first = s // STEPS_PER_BATCH, STEP * (s % STEPS_PER_BATCH)
+            nc.sync.dma_start(
+                out=kf[b, :, first : first + STEP, :].rearrange("h (p j) d -> p h (j d)", j=TILES),
+                in_=kf_rows[s][:].rearrange("p h j d -> p h (j d)"),
+            )
+            nc.sync.dma_start(
+                out=v[b, :, first : first + STEP, :].rearrange("h (p j) d -> p h (j d)", j=TILES),
+                in_=v_rows[:].rearrange("p h j d -> p h (j d)"),
+            )
+
+        def run(stage, s):
+            if 0 <= s < STEPS:
+                stage(s)
+
+        for r in range(STEPS + 4):
+            run(store, r - 4)
+            run(rotate, r - 2)
+            run(quantise_c, r - 3)
+            run(quantise_x, r)
+            run(compress, r - 1)
+            run(transpose_c, r - 2)
+            run(expand, r - 3)

@@ -28,8 +28,6 @@ BASE = 10000.0
 
 FLOPS = 2 * B * N * (E * CKV + KVR * H * (NOPE + VDIM))
 
-TWO_PI_HI = 6.28125
-TWO_PI_LO = 2.0 * math.pi - TWO_PI_HI
 ROUND_MAGIC = 1.5 * 2.0**23
 
 
@@ -99,36 +97,30 @@ def tile_multilatentattention_pb_t_kernel(
             nc.vector.tensor_scalar_mul(theta[:, width : 2 * width], theta[:, 0:width], ratio**width)
             width *= 2
 
-        angle = const.tile([P, TABLE], F32)
-        nc.vector.tensor_tensor(
-            out=angle[:].rearrange("p (n i) -> p n i", i=PAIRS),
-            in0=position[:].unsqueeze(2).to_broadcast([P, STEPS_PER_BATCH * TILES, PAIRS]),
-            in1=theta[:].unsqueeze(1).to_broadcast([P, STEPS_PER_BATCH * TILES, PAIRS]),
-            op=ALU.mult,
-        )
         turns = const.tile([P, TABLE], F32)
-        nc.vector.tensor_scalar(
-            out=turns[:], in0=angle[:], scalar1=0.5 / math.pi, scalar2=ROUND_MAGIC, op0=ALU.mult, op1=ALU.add
+        nc.vector.scalar_tensor_tensor(
+            out=turns[:].rearrange("p (n i) -> p n i", i=PAIRS),
+            in0=position[:].unsqueeze(2).to_broadcast([P, STEPS_PER_BATCH * TILES, PAIRS]),
+            scalar=0.5 / math.pi,
+            in1=theta[:].unsqueeze(1).to_broadcast([P, STEPS_PER_BATCH * TILES, PAIRS]),
+            op0=ALU.mult,
+            op1=ALU.mult,
         )
         whole_turns = const.tile([P, TABLE], F32)
-        nc.vector.tensor_scalar_add(whole_turns[:], turns[:], -ROUND_MAGIC)
-        partly_reduced = const.tile([P, TABLE], F32)
-        nc.vector.scalar_tensor_tensor(
-            out=partly_reduced[:], in0=whole_turns[:], scalar=-TWO_PI_HI, in1=angle[:], op0=ALU.mult, op1=ALU.add
+        nc.vector.tensor_scalar(
+            out=whole_turns[:], in0=turns[:], scalar1=ROUND_MAGIC, scalar2=-ROUND_MAGIC, op0=ALU.add, op1=ALU.add
         )
-        reduced = const.tile([P, TABLE], F32)
-        nc.vector.scalar_tensor_tensor(
-            out=reduced[:], in0=whole_turns[:], scalar=-TWO_PI_LO, in1=partly_reduced[:], op0=ALU.mult, op1=ALU.add
-        )
+        part_turn = const.tile([P, TABLE], F32)
+        nc.vector.tensor_tensor(out=part_turn[:], in0=turns[:], in1=whole_turns[:], op=ALU.subtract)
         sin_half = const.tile([P, TABLE], F32)
-        nc.scalar.activation(out=sin_half[:], in_=reduced[:], func=ACT.Sin, scale=0.5)
+        nc.scalar.activation(out=sin_half[:], in_=part_turn[:], func=ACT.Sin, scale=math.pi)
         minus_abs = const.tile([P, TABLE], F32)
         nc.vector.scalar_tensor_tensor(
-            out=minus_abs[:], in0=reduced[:], scalar=-1.0, in1=reduced[:], op0=ALU.mult, op1=ALU.min
+            out=minus_abs[:], in0=part_turn[:], scalar=-1.0, in1=part_turn[:], op0=ALU.mult, op1=ALU.min
         )
         cos_arg = const.tile([P, TABLE], F32)
         nc.vector.tensor_scalar(
-            out=cos_arg[:], in0=minus_abs[:], scalar1=0.5, scalar2=0.5 * math.pi, op0=ALU.mult, op1=ALU.add
+            out=cos_arg[:], in0=minus_abs[:], scalar1=math.pi, scalar2=0.5 * math.pi, op0=ALU.mult, op1=ALU.add
         )
         cos_half = const.tile([P, TABLE], F32)
         nc.scalar.activation(out=cos_half[:], in_=cos_arg[:], func=ACT.Sin)
@@ -278,6 +270,6 @@ def tile_multilatentattention_pb_t_kernel(
             run(rotate, r - 2)
             run(quantise_c, r - 3)
             run(quantise_x, r)
-            run(compress, r - 1)
             run(transpose_c, r - 2)
+            run(compress, r - 1)
             run(expand, r - 3)

@@ -78,16 +78,13 @@ def tile_multilatentattention_pb_t_kernel(
         for s in range(2, STEPS):
             load_x(s)
 
-        identity = const.tile([P, P], F32)
-        make_identity(nc, identity[:])
-
         TABLE = STEPS_PER_BATCH * TILES * PAIRS
         position_int = const.tile([P, STEPS_PER_BATCH * TILES], I32)
         nc.gpsimd.iota(
             position_int[:], pattern=[[STEP, STEPS_PER_BATCH], [1, TILES]], base=0, channel_multiplier=TILES
         )
-        position = const.tile([P, STEPS_PER_BATCH * TILES], F32)
-        nc.vector.tensor_copy(out=position[:], in_=position_int[:])
+        identity = const.tile([P, P], F32)
+        make_identity(nc, identity[:])
 
         ratio = BASE ** (-2.0 / ROPE)
         theta = const.tile([P, PAIRS], F32)
@@ -96,6 +93,8 @@ def tile_multilatentattention_pb_t_kernel(
         while width < PAIRS:
             nc.vector.tensor_scalar_mul(theta[:, width : 2 * width], theta[:, 0:width], ratio**width)
             width *= 2
+        position = const.tile([P, STEPS_PER_BATCH * TILES], F32)
+        nc.vector.tensor_copy(out=position[:], in_=position_int[:])
 
         turns = const.tile([P, TABLE], F32)
         nc.vector.scalar_tensor_tensor(
@@ -112,32 +111,29 @@ def tile_multilatentattention_pb_t_kernel(
         )
         part_turn = const.tile([P, TABLE], F32)
         nc.vector.tensor_tensor(out=part_turn[:], in0=turns[:], in1=whole_turns[:], op=ALU.subtract)
-        sin_half = const.tile([P, TABLE], F32)
-        nc.scalar.activation(out=sin_half[:], in_=part_turn[:], func=ACT.Sin, scale=math.pi)
+        sin_table = const.tile([P, STEPS_PER_BATCH, TILES, PAIRS], F32)
+        nc.scalar.activation(
+            out=sin_table[:].rearrange("p r j i -> p (r j i)"), in_=part_turn[:], func=ACT.Sin, scale=2.0 * math.pi
+        )
         minus_abs = const.tile([P, TABLE], F32)
         nc.vector.scalar_tensor_tensor(
             out=minus_abs[:], in0=part_turn[:], scalar=-1.0, in1=part_turn[:], op0=ALU.mult, op1=ALU.min
         )
         cos_arg = const.tile([P, TABLE], F32)
         nc.vector.tensor_scalar(
-            out=cos_arg[:], in0=minus_abs[:], scalar1=math.pi, scalar2=0.5 * math.pi, op0=ALU.mult, op1=ALU.add
-        )
-        cos_half = const.tile([P, TABLE], F32)
-        nc.scalar.activation(out=cos_half[:], in_=cos_arg[:], func=ACT.Sin)
-        minus_two_sq = const.tile([P, TABLE], F32)
-        nc.vector.scalar_tensor_tensor(
-            out=minus_two_sq[:], in0=sin_half[:], scalar=-2.0, in1=sin_half[:], op0=ALU.mult, op1=ALU.mult
+            out=cos_arg[:], in0=minus_abs[:], scalar1=2.0 * math.pi, scalar2=0.5 * math.pi, op0=ALU.mult, op1=ALU.add
         )
         cos_table = const.tile([P, STEPS_PER_BATCH, TILES, PAIRS], F32)
-        nc.vector.tensor_scalar_add(cos_table[:].rearrange("p r j i -> p (r j i)"), minus_two_sq[:], 1.0)
-        sin_table = const.tile([P, STEPS_PER_BATCH, TILES, PAIRS], F32)
-        nc.vector.scalar_tensor_tensor(
-            out=sin_table[:].rearrange("p r j i -> p (r j i)"),
-            in0=sin_half[:], scalar=2.0, in1=cos_half[:], op0=ALU.mult, op1=ALU.mult,
-        )
+        nc.scalar.activation(out=cos_table[:].rearrange("p r j i -> p (r j i)"), in_=cos_arg[:], func=ACT.Sin)
 
         x_codes, x_scales, pe_sums, c_rounded = {}, {}, {}, {}
         c_grouped, c_codes, c_scales, kv_sums, kf_rows = {}, {}, {}, {}, {}
+
+        def copy_out(j, out, in_):
+            if j == 0:
+                nc.scalar.copy(out=out, in_=in_)
+            else:
+                nc.vector.tensor_copy(out=out, in_=in_)
 
         def quantise_x(s):
             grouped = work.tile([P, TILES, X_PASSES, P, PACK], BF16, name="x_grouped", align_bytes=64)
@@ -149,9 +145,7 @@ def tile_multilatentattention_pb_t_kernel(
                         nc.tensor.transpose(
                             flipped[:, g, u, :], words[:, 2 * P * g + u : 2 * P * (g + 1) : 2], identity[:]
                         )
-                nc.scalar.copy(
-                    out=grouped[:, j].bitcast(F32), in_=flipped[:].rearrange("p g u t -> p g t u")
-                )
+                copy_out(j, grouped[:, j].bitcast(F32), flipped[:].rearrange("p g u t -> p g t u"))
             x_codes[s] = work.tile([P, TILES, X_PASSES, P], U32, name="x_codes", align_bytes=64)
             x_scales[s] = work.tile([P, TILES, X_PASSES, P], U8, name="x_scales", align_bytes=64)
             nc.vector.quantize_mx(
@@ -221,15 +215,19 @@ def tile_multilatentattention_pb_t_kernel(
             )
             nc.vector.tensor_tensor(out=with_sin[:, :, 1, :], in0=pe[:, :, 0, :], in1=sin, op=ALU.mult)
             kf_rows[s] = result.tile([P, H, TILES, KF], F32, name="kf_rows")
-            nc.vector.tensor_tensor(
+            nc.gpsimd.tensor_tensor(
                 out=kf_rows[s][:, 0, :, NOPE:KF].rearrange("p j (i e) -> p j i e", e=2),
                 in0=with_cos[:].rearrange("p j e i -> p j i e"),
                 in1=with_sin[:].rearrange("p j e i -> p j i e"),
                 op=ALU.add,
             )
-            nc.vector.tensor_copy(
+            nc.gpsimd.tensor_scalar(
                 out=kf_rows[s][:, 1:H, :, NOPE:KF],
-                in_=kf_rows[s][:, 0:1, :, NOPE:KF].to_broadcast([P, H - 1, TILES, ROPE]),
+                in0=kf_rows[s][:, 0:1, :, NOPE:KF].to_broadcast([P, H - 1, TILES, ROPE]),
+                scalar1=1.0,
+                scalar2=0.0,
+                op0=ALU.mult,
+                op1=ALU.add,
             )
 
         def expand(s):
@@ -247,10 +245,9 @@ def tile_multilatentattention_pb_t_kernel(
 
         def store(s):
             v_rows = result.tile([P, H, TILES, VDIM], F32, name="v_rows")
-            nc.vector.tensor_copy(out=kf_rows[s][:, :, 0, 0:NOPE], in_=kv_sums[s, 0][:, :, 0, :])
-            nc.vector.tensor_copy(out=v_rows[:, :, 0, :], in_=kv_sums[s, 0][:, :, 1, :])
-            nc.scalar.copy(out=kf_rows[s][:, :, 1, 0:NOPE], in_=kv_sums[s, 1][:, :, 0, :])
-            nc.scalar.copy(out=v_rows[:, :, 1, :], in_=kv_sums[s, 1][:, :, 1, :])
+            for j in range(TILES):
+                copy_out(j, kf_rows[s][:, :, j, 0:NOPE], kv_sums[s, j][:, :, 0, :])
+                copy_out(j, v_rows[:, :, j, :], kv_sums[s, j][:, :, 1, :])
             b, first = s // STEPS_PER_BATCH, STEP * (s % STEPS_PER_BATCH)
             nc.sync.dma_start(
                 out=kf[b, :, first : first + STEP, :].rearrange("h (p j) d -> p h (j d)", j=TILES),
@@ -266,8 +263,8 @@ def tile_multilatentattention_pb_t_kernel(
                 stage(s)
 
         for r in range(STEPS + 4):
-            run(store, r - 4)
             run(rotate, r - 2)
+            run(store, r - 4)
             run(quantise_c, r - 3)
             run(quantise_x, r)
             run(transpose_c, r - 2)

@@ -56,6 +56,7 @@ def tile_multilatentattention_pb_t_kernel(
             nc.sync.dma_start(out=x_all[:, s], in_=x_rows[:, s])
 
         load_x(0)
+        load_x(1)
         for quad in range(4):
             nc.sync.dma_start(
                 out=wa_scales[32 * quad : 32 * quad + 4].bitcast(I32),
@@ -65,7 +66,6 @@ def tile_multilatentattention_pb_t_kernel(
             out=wa_words[:].bitcast(I32),
             in_=Wkva_words.rearrange("g p n t -> p g (n t)").bitcast(I32),
         )
-        load_x(1)
         for quad in range(4):
             nc.sync.dma_start(
                 out=wb_scales[32 * quad : 32 * quad + 4].bitcast(I32),
@@ -78,74 +78,26 @@ def tile_multilatentattention_pb_t_kernel(
         for s in range(2, STEPS):
             load_x(s)
 
-        TABLE = STEPS_PER_BATCH * TILES * PAIRS
-        position_int = const.tile([P, STEPS_PER_BATCH * TILES], I32)
-        nc.gpsimd.iota(
-            position_int[:], pattern=[[STEP, STEPS_PER_BATCH], [1, TILES]], base=0, channel_multiplier=TILES
-        )
-        identity = const.tile([P, P], F32)
-        make_identity(nc, identity[:])
-
-        ratio = BASE ** (-2.0 / ROPE)
-        theta = const.tile([P, PAIRS], F32)
-        nc.vector.memset(theta[:, 0:1], 1.0)
-        width = 1
-        while width < PAIRS:
-            nc.vector.tensor_scalar_mul(theta[:, width : 2 * width], theta[:, 0:width], ratio**width)
-            width *= 2
-        position = const.tile([P, STEPS_PER_BATCH * TILES], F32)
-        nc.vector.tensor_copy(out=position[:], in_=position_int[:])
-
-        turns = const.tile([P, TABLE], F32)
-        nc.vector.scalar_tensor_tensor(
-            out=turns[:].rearrange("p (n i) -> p n i", i=PAIRS),
-            in0=position[:].unsqueeze(2).to_broadcast([P, STEPS_PER_BATCH * TILES, PAIRS]),
-            scalar=0.5 / math.pi,
-            in1=theta[:].unsqueeze(1).to_broadcast([P, STEPS_PER_BATCH * TILES, PAIRS]),
-            op0=ALU.mult,
-            op1=ALU.mult,
-        )
-        whole_turns = const.tile([P, TABLE], F32)
-        nc.vector.tensor_scalar(
-            out=whole_turns[:], in0=turns[:], scalar1=ROUND_MAGIC, scalar2=-ROUND_MAGIC, op0=ALU.add, op1=ALU.add
-        )
-        part_turn = const.tile([P, TABLE], F32)
-        nc.vector.tensor_tensor(out=part_turn[:], in0=turns[:], in1=whole_turns[:], op=ALU.subtract)
-        sin_table = const.tile([P, STEPS_PER_BATCH, TILES, PAIRS], F32)
-        nc.scalar.activation(
-            out=sin_table[:].rearrange("p r j i -> p (r j i)"), in_=part_turn[:], func=ACT.Sin, scale=2.0 * math.pi
-        )
-        minus_abs = const.tile([P, TABLE], F32)
-        nc.vector.scalar_tensor_tensor(
-            out=minus_abs[:], in0=part_turn[:], scalar=-1.0, in1=part_turn[:], op0=ALU.mult, op1=ALU.min
-        )
-        cos_arg = const.tile([P, TABLE], F32)
-        nc.vector.tensor_scalar(
-            out=cos_arg[:], in0=minus_abs[:], scalar1=2.0 * math.pi, scalar2=0.5 * math.pi, op0=ALU.mult, op1=ALU.add
-        )
-        cos_table = const.tile([P, STEPS_PER_BATCH, TILES, PAIRS], F32)
-        nc.scalar.activation(out=cos_table[:].rearrange("p r j i -> p (r j i)"), in_=cos_arg[:], func=ACT.Sin)
-
-        x_codes, x_scales, pe_sums, c_rounded = {}, {}, {}, {}
+        x_sorted, x_codes, x_scales, pe_sums, c_rounded = {}, {}, {}, {}, {}
         c_grouped, c_codes, c_scales, kv_sums, kf_rows = {}, {}, {}, {}, {}
 
-        def copy_out(j, out, in_):
-            if j == 0:
-                nc.scalar.copy(out=out, in_=in_)
-            else:
-                nc.vector.tensor_copy(out=out, in_=in_)
+        def sort_x(s):
+            x_sorted[s] = work.tile([P, TILES, X_PASSES, 2, P], F32, name="x_sorted")
+            nc.vector.tensor_copy(
+                out=x_sorted[s][:],
+                in_=x_all[:, s].bitcast(F32).rearrange("p j (g q u) -> p j g u q", g=X_PASSES, u=2),
+            )
 
         def quantise_x(s):
             grouped = work.tile([P, TILES, X_PASSES, P, PACK], BF16, name="x_grouped", align_bytes=64)
             for j in range(TILES):
-                words = x_all[:, s, j, :].bitcast(F32)
                 flipped = psum.tile([P, X_PASSES, 2, P], F32, name="x_flipped", bufs=2)
                 for g in range(X_PASSES):
                     for u in range(2):
-                        nc.tensor.transpose(
-                            flipped[:, g, u, :], words[:, 2 * P * g + u : 2 * P * (g + 1) : 2], identity[:]
-                        )
-                copy_out(j, grouped[:, j].bitcast(F32), flipped[:].rearrange("p g u t -> p g t u"))
+                        nc.tensor.transpose(flipped[:, g, u, :], x_sorted[s][:, j, g, u, :], identity[:])
+                nc.scalar.copy(
+                    out=grouped[:, j].bitcast(F32), in_=flipped[:].rearrange("p g u t -> p g t u")
+                )
             x_codes[s] = work.tile([P, TILES, X_PASSES, P], U32, name="x_codes", align_bytes=64)
             x_scales[s] = work.tile([P, TILES, X_PASSES, P], U8, name="x_scales", align_bytes=64)
             nc.vector.quantize_mx(
@@ -245,9 +197,10 @@ def tile_multilatentattention_pb_t_kernel(
 
         def store(s):
             v_rows = result.tile([P, H, TILES, VDIM], F32, name="v_rows")
-            for j in range(TILES):
-                copy_out(j, kf_rows[s][:, :, j, 0:NOPE], kv_sums[s, j][:, :, 0, :])
-                copy_out(j, v_rows[:, :, j, :], kv_sums[s, j][:, :, 1, :])
+            nc.scalar.copy(out=kf_rows[s][:, :, 0, 0:NOPE], in_=kv_sums[s, 0][:, :, 0, :])
+            nc.scalar.copy(out=v_rows[:, :, 0, :], in_=kv_sums[s, 0][:, :, 1, :])
+            nc.vector.tensor_copy(out=kf_rows[s][:, :, 1, 0:NOPE], in_=kv_sums[s, 1][:, :, 0, :])
+            nc.vector.tensor_copy(out=v_rows[:, :, 1, :], in_=kv_sums[s, 1][:, :, 1, :])
             b, first = s // STEPS_PER_BATCH, STEP * (s % STEPS_PER_BATCH)
             nc.sync.dma_start(
                 out=kf[b, :, first : first + STEP, :].rearrange("h (p j) d -> p h (j d)", j=TILES),
@@ -258,14 +211,62 @@ def tile_multilatentattention_pb_t_kernel(
                 in_=v_rows[:].rearrange("p h j d -> p h (j d)"),
             )
 
+        TABLE = STEPS_PER_BATCH * TILES * PAIRS
+        position_int = const.tile([P, STEPS_PER_BATCH * TILES], I32)
+        nc.gpsimd.iota(
+            position_int[:], pattern=[[STEP, STEPS_PER_BATCH], [1, TILES]], base=0, channel_multiplier=TILES
+        )
+        identity = const.tile([P, P], F32)
+        make_identity(nc, identity[:])
+
+        position = const.tile([P, STEPS_PER_BATCH * TILES], F32)
+        nc.vector.tensor_copy(out=position[:], in_=position_int[:])
+
+        ratio = BASE ** (-2.0 / ROPE)
+        turns = const.tile([P, STEPS_PER_BATCH * TILES, PAIRS], F32)
+        nc.vector.tensor_scalar_mul(turns[:, :, 0], position[:], 0.5 / math.pi)
+        width = 1
+        while width < PAIRS:
+            nc.vector.tensor_scalar_mul(turns[:, :, width : 2 * width], turns[:, :, 0:width], ratio**width)
+            width *= 2
+        whole_turns = const.tile([P, TABLE], F32)
+        nc.vector.tensor_scalar(
+            out=whole_turns[:],
+            in0=turns[:].rearrange("p n i -> p (n i)"),
+            scalar1=ROUND_MAGIC,
+            scalar2=-ROUND_MAGIC,
+            op0=ALU.add,
+            op1=ALU.add,
+        )
+        part_turn = const.tile([P, TABLE], F32)
+        nc.vector.tensor_tensor(
+            out=part_turn[:], in0=turns[:].rearrange("p n i -> p (n i)"), in1=whole_turns[:], op=ALU.subtract
+        )
+        sort_x(0)
+        sin_table = const.tile([P, STEPS_PER_BATCH, TILES, PAIRS], F32)
+        nc.scalar.activation(
+            out=sin_table[:].rearrange("p r j i -> p (r j i)"), in_=part_turn[:], func=ACT.Sin, scale=2.0 * math.pi
+        )
+        minus_abs = const.tile([P, TABLE], F32)
+        nc.vector.scalar_tensor_tensor(
+            out=minus_abs[:], in0=part_turn[:], scalar=-1.0, in1=part_turn[:], op0=ALU.mult, op1=ALU.min
+        )
+        cos_arg = const.tile([P, TABLE], F32)
+        nc.vector.tensor_scalar(
+            out=cos_arg[:], in0=minus_abs[:], scalar1=2.0 * math.pi, scalar2=0.5 * math.pi, op0=ALU.mult, op1=ALU.add
+        )
+        cos_table = const.tile([P, STEPS_PER_BATCH, TILES, PAIRS], F32)
+        nc.scalar.activation(out=cos_table[:].rearrange("p r j i -> p (r j i)"), in_=cos_arg[:], func=ACT.Sin)
+
         def run(stage, s):
             if 0 <= s < STEPS:
                 stage(s)
 
         for r in range(STEPS + 4):
+            run(sort_x, r + 1)
             run(rotate, r - 2)
-            run(store, r - 4)
             run(quantise_c, r - 3)
+            run(store, r - 4)
             run(quantise_x, r)
             run(transpose_c, r - 2)
             run(compress, r - 1)

@@ -78,6 +78,9 @@ def tile_multilatentattention_pb_t_kernel(
         for s in range(2, STEPS):
             load_x(s)
 
+        identity = const.tile([P, P], F32)
+        make_identity(nc, identity[:])
+
         x_sorted, x_codes, x_scales, pe_sums, c_rounded = {}, {}, {}, {}, {}
         c_grouped, c_codes, c_scales, kv_sums, kf_rows = {}, {}, {}, {}, {}
 
@@ -140,9 +143,8 @@ def tile_multilatentattention_pb_t_kernel(
                         identity[:],
                     )
             c_grouped[s] = work.tile([P, TILES, P, PACK], BF16, name="c_grouped", align_bytes=64)
-            nc.scalar.copy(
-                out=c_grouped[s][:].bitcast(F32), in_=flipped[:].rearrange("p j u t -> p j t u")
-            )
+            copy = nc.scalar.copy if s % 2 == 0 else nc.vector.tensor_copy
+            copy(out=c_grouped[s][:].bitcast(F32), in_=flipped[:].rearrange("p j u t -> p j t u"))
 
         def quantise_c(s):
             c_codes[s] = work.tile([P, TILES, P], U32, name="c_codes", align_bytes=64)
@@ -173,13 +175,11 @@ def tile_multilatentattention_pb_t_kernel(
                 in1=with_sin[:].rearrange("p j e i -> p j i e"),
                 op=ALU.add,
             )
-            nc.gpsimd.tensor_scalar(
-                out=kf_rows[s][:, 1:H, :, NOPE:KF],
-                in0=kf_rows[s][:, 0:1, :, NOPE:KF].to_broadcast([P, H - 1, TILES, ROPE]),
-                scalar1=1.0,
-                scalar2=0.0,
-                op0=ALU.mult,
-                op1=ALU.add,
+            scale_and_add(
+                kf_rows[s][:, 1:H, :, NOPE:KF],
+                kf_rows[s][:, 0:1, :, NOPE:KF].to_broadcast([P, H - 1, TILES, ROPE]),
+                1.0,
+                0.0,
             )
 
         def expand(s):
@@ -211,58 +211,51 @@ def tile_multilatentattention_pb_t_kernel(
                 in_=v_rows[:].rearrange("p h j d -> p h (j d)"),
             )
 
-        TABLE = STEPS_PER_BATCH * TILES * PAIRS
-        position_int = const.tile([P, STEPS_PER_BATCH * TILES], I32)
-        nc.gpsimd.iota(
-            position_int[:], pattern=[[STEP, STEPS_PER_BATCH], [1, TILES]], base=0, channel_multiplier=TILES
-        )
-        identity = const.tile([P, P], F32)
-        make_identity(nc, identity[:])
-
-        position = const.tile([P, STEPS_PER_BATCH * TILES], F32)
-        nc.vector.tensor_copy(out=position[:], in_=position_int[:])
-
-        ratio = BASE ** (-2.0 / ROPE)
-        turns = const.tile([P, STEPS_PER_BATCH * TILES, PAIRS], F32)
-        nc.vector.tensor_scalar_mul(turns[:, :, 0], position[:], 0.5 / math.pi)
-        width = 1
-        while width < PAIRS:
-            nc.vector.tensor_scalar_mul(turns[:, :, width : 2 * width], turns[:, :, 0:width], ratio**width)
-            width *= 2
-        whole_turns = const.tile([P, TABLE], F32)
-        nc.vector.tensor_scalar(
-            out=whole_turns[:],
-            in0=turns[:].rearrange("p n i -> p (n i)"),
-            scalar1=ROUND_MAGIC,
-            scalar2=-ROUND_MAGIC,
-            op0=ALU.add,
-            op1=ALU.add,
-        )
-        part_turn = const.tile([P, TABLE], F32)
-        nc.vector.tensor_tensor(
-            out=part_turn[:], in0=turns[:].rearrange("p n i -> p (n i)"), in1=whole_turns[:], op=ALU.subtract
-        )
-        sort_x(0)
-        sin_table = const.tile([P, STEPS_PER_BATCH, TILES, PAIRS], F32)
-        nc.scalar.activation(
-            out=sin_table[:].rearrange("p r j i -> p (r j i)"), in_=part_turn[:], func=ACT.Sin, scale=2.0 * math.pi
-        )
-        minus_abs = const.tile([P, TABLE], F32)
-        nc.vector.scalar_tensor_tensor(
-            out=minus_abs[:], in0=part_turn[:], scalar=-1.0, in1=part_turn[:], op0=ALU.mult, op1=ALU.min
-        )
-        cos_arg = const.tile([P, TABLE], F32)
-        nc.vector.tensor_scalar(
-            out=cos_arg[:], in0=minus_abs[:], scalar1=2.0 * math.pi, scalar2=0.5 * math.pi, op0=ALU.mult, op1=ALU.add
-        )
         cos_table = const.tile([P, STEPS_PER_BATCH, TILES, PAIRS], F32)
-        nc.scalar.activation(out=cos_table[:].rearrange("p r j i -> p (r j i)"), in_=cos_arg[:], func=ACT.Sin)
+        sin_table = const.tile([P, STEPS_PER_BATCH, TILES, PAIRS], F32)
+
+        def scale_and_add(out, in_, scale, addend):
+            nc.gpsimd.tensor_scalar(out=out, in0=in_, scalar1=scale, scalar2=addend, op0=ALU.mult, op1=ALU.add)
+
+        def build_tables():
+            positions = STEPS_PER_BATCH * TILES
+            position = const.tile([P, positions], F32)
+            nc.gpsimd.iota(
+                position[:],
+                pattern=[[STEP, STEPS_PER_BATCH], [1, TILES]],
+                base=0,
+                channel_multiplier=TILES,
+                allow_small_or_imprecise_dtypes=True,
+            )
+            ratio = BASE ** (-2.0 / ROPE)
+            turns = const.tile([P, positions, PAIRS], F32)
+            scale_and_add(turns[:, :, 0], position[:], 0.5 / math.pi, 0.0)
+            width = 1
+            while width < PAIRS:
+                scale_and_add(turns[:, :, width : 2 * width], turns[:, :, 0:width], ratio**width, 0.0)
+                width *= 2
+            shifted = const.tile([P, positions * PAIRS], F32)
+            scale_and_add(shifted[:], turns[:].rearrange("p n i -> p (n i)"), 1.0, ROUND_MAGIC)
+            whole_turns = const.tile([P, positions * PAIRS], F32)
+            scale_and_add(whole_turns[:], shifted[:], 1.0, -ROUND_MAGIC)
+            part_turn = const.tile([P, positions * PAIRS], F32)
+            nc.gpsimd.tensor_tensor(
+                out=part_turn[:], in0=turns[:].rearrange("p n i -> p (n i)"), in1=whole_turns[:], op=ALU.subtract
+            )
+            nc.scalar.activation(
+                out=sin_table[:].rearrange("p r j i -> p (r j i)"), in_=part_turn[:], func=ACT.Sin, scale=2.0 * math.pi
+            )
+            sin_half = const.tile([P, positions * PAIRS], F32)
+            nc.scalar.activation(out=sin_half[:], in_=part_turn[:], func=ACT.Sin, scale=math.pi)
+            sin_half_squared = const.tile([P, positions * PAIRS], F32)
+            nc.gpsimd.tensor_tensor(out=sin_half_squared[:], in0=sin_half[:], in1=sin_half[:], op=ALU.mult)
+            scale_and_add(cos_table[:].rearrange("p r j i -> p (r j i)"), sin_half_squared[:], -2.0, 1.0)
 
         def run(stage, s):
             if 0 <= s < STEPS:
                 stage(s)
 
-        for r in range(STEPS + 4):
+        def pipeline_round(r):
             run(sort_x, r + 1)
             run(rotate, r - 2)
             run(quantise_c, r - 3)
@@ -271,3 +264,9 @@ def tile_multilatentattention_pb_t_kernel(
             run(transpose_c, r - 2)
             run(compress, r - 1)
             run(expand, r - 3)
+
+        sort_x(0)
+        pipeline_round(0)
+        build_tables()
+        for r in range(1, STEPS + 4):
+            pipeline_round(r)

@@ -78,9 +78,6 @@ def tile_multilatentattention_pb_t_kernel(
         for s in range(2, STEPS):
             load_x(s)
 
-        identity = const.tile([P, P], F32)
-        make_identity(nc, identity[:])
-
         x_sorted, x_codes, x_scales, pe_sums, c_rounded = {}, {}, {}, {}, {}
         c_grouped, c_codes, c_scales, kv_sums, kf_rows = {}, {}, {}, {}, {}
 
@@ -143,8 +140,9 @@ def tile_multilatentattention_pb_t_kernel(
                         identity[:],
                     )
             c_grouped[s] = work.tile([P, TILES, P, PACK], BF16, name="c_grouped", align_bytes=64)
-            copy = nc.scalar.copy if s % 2 == 0 else nc.vector.tensor_copy
-            copy(out=c_grouped[s][:].bitcast(F32), in_=flipped[:].rearrange("p j u t -> p j t u"))
+            nc.scalar.copy(
+                out=c_grouped[s][:].bitcast(F32), in_=flipped[:].rearrange("p j u t -> p j t u")
+            )
 
         def quantise_c(s):
             c_codes[s] = work.tile([P, TILES, P], U32, name="c_codes", align_bytes=64)
@@ -175,11 +173,13 @@ def tile_multilatentattention_pb_t_kernel(
                 in1=with_sin[:].rearrange("p j e i -> p j i e"),
                 op=ALU.add,
             )
-            scale_and_add(
-                kf_rows[s][:, 1:H, :, NOPE:KF],
-                kf_rows[s][:, 0:1, :, NOPE:KF].to_broadcast([P, H - 1, TILES, ROPE]),
-                1.0,
-                0.0,
+            nc.gpsimd.tensor_scalar(
+                out=kf_rows[s][:, 1:H, :, NOPE:KF],
+                in0=kf_rows[s][:, 0:1, :, NOPE:KF].to_broadcast([P, H - 1, TILES, ROPE]),
+                scalar1=1.0,
+                scalar2=0.0,
+                op0=ALU.mult,
+                op1=ALU.add,
             )
 
         def expand(s):
@@ -211,45 +211,43 @@ def tile_multilatentattention_pb_t_kernel(
                 in_=v_rows[:].rearrange("p h j d -> p h (j d)"),
             )
 
-        cos_table = const.tile([P, STEPS_PER_BATCH, TILES, PAIRS], F32)
+        TABLE = STEPS_PER_BATCH * TILES * PAIRS
+        position_int = const.tile([P, STEPS_PER_BATCH * TILES], I32)
+        nc.gpsimd.iota(
+            position_int[:], pattern=[[STEP, STEPS_PER_BATCH], [1, TILES]], base=0, channel_multiplier=TILES
+        )
+        identity = const.tile([P, P], F32)
+        make_identity(nc, identity[:])
+
+        position = const.tile([P, STEPS_PER_BATCH * TILES], F32)
+        nc.vector.tensor_copy(out=position[:], in_=position_int[:])
+
+        ratio = BASE ** (-2.0 / ROPE)
+        turns = const.tile([P, STEPS_PER_BATCH * TILES, PAIRS], F32)
+        nc.vector.tensor_scalar_mul(turns[:, :, 0], position[:], 0.5 / math.pi)
+        width = 1
+        while width < PAIRS:
+            nc.vector.tensor_scalar_mul(turns[:, :, width : 2 * width], turns[:, :, 0:width], ratio**width)
+            width *= 2
+        whole_turns = const.tile([P, TABLE], F32)
+        nc.vector.tensor_scalar(
+            out=whole_turns[:],
+            in0=turns[:].rearrange("p n i -> p (n i)"),
+            scalar1=ROUND_MAGIC,
+            scalar2=-ROUND_MAGIC,
+            op0=ALU.add,
+            op1=ALU.add,
+        )
+        part_turn = const.tile([P, TABLE], F32)
+        nc.vector.tensor_tensor(
+            out=part_turn[:], in0=turns[:].rearrange("p n i -> p (n i)"), in1=whole_turns[:], op=ALU.subtract
+        )
         sin_table = const.tile([P, STEPS_PER_BATCH, TILES, PAIRS], F32)
-
-        def scale_and_add(out, in_, scale, addend):
-            nc.gpsimd.tensor_scalar(out=out, in0=in_, scalar1=scale, scalar2=addend, op0=ALU.mult, op1=ALU.add)
-
-        def build_tables():
-            positions = STEPS_PER_BATCH * TILES
-            position = const.tile([P, positions], F32)
-            nc.gpsimd.iota(
-                position[:],
-                pattern=[[STEP, STEPS_PER_BATCH], [1, TILES]],
-                base=0,
-                channel_multiplier=TILES,
-                allow_small_or_imprecise_dtypes=True,
-            )
-            ratio = BASE ** (-2.0 / ROPE)
-            turns = const.tile([P, positions, PAIRS], F32)
-            scale_and_add(turns[:, :, 0], position[:], 0.5 / math.pi, 0.0)
-            width = 1
-            while width < PAIRS:
-                scale_and_add(turns[:, :, width : 2 * width], turns[:, :, 0:width], ratio**width, 0.0)
-                width *= 2
-            shifted = const.tile([P, positions * PAIRS], F32)
-            scale_and_add(shifted[:], turns[:].rearrange("p n i -> p (n i)"), 1.0, ROUND_MAGIC)
-            whole_turns = const.tile([P, positions * PAIRS], F32)
-            scale_and_add(whole_turns[:], shifted[:], 1.0, -ROUND_MAGIC)
-            part_turn = const.tile([P, positions * PAIRS], F32)
-            nc.gpsimd.tensor_tensor(
-                out=part_turn[:], in0=turns[:].rearrange("p n i -> p (n i)"), in1=whole_turns[:], op=ALU.subtract
-            )
-            nc.scalar.activation(
-                out=sin_table[:].rearrange("p r j i -> p (r j i)"), in_=part_turn[:], func=ACT.Sin, scale=2.0 * math.pi
-            )
-            sin_half = const.tile([P, positions * PAIRS], F32)
-            nc.scalar.activation(out=sin_half[:], in_=part_turn[:], func=ACT.Sin, scale=math.pi)
-            sin_half_squared = const.tile([P, positions * PAIRS], F32)
-            nc.gpsimd.tensor_tensor(out=sin_half_squared[:], in0=sin_half[:], in1=sin_half[:], op=ALU.mult)
-            scale_and_add(cos_table[:].rearrange("p r j i -> p (r j i)"), sin_half_squared[:], -2.0, 1.0)
+        nc.scalar.activation(
+            out=sin_table[:].rearrange("p r j i -> p (r j i)"), in_=part_turn[:], func=ACT.Sin, scale=2.0 * math.pi
+        )
+        sin_half = const.tile([P, TABLE], F32)
+        nc.scalar.activation(out=sin_half[:], in_=part_turn[:], func=ACT.Sin, scale=math.pi)
 
         def run(stage, s):
             if 0 <= s < STEPS:
@@ -267,6 +265,11 @@ def tile_multilatentattention_pb_t_kernel(
 
         sort_x(0)
         pipeline_round(0)
-        build_tables()
+        minus_two_squares = const.tile([P, TABLE], F32)
+        nc.vector.scalar_tensor_tensor(
+            out=minus_two_squares[:], in0=sin_half[:], scalar=-2.0, in1=sin_half[:], op0=ALU.mult, op1=ALU.mult
+        )
+        cos_table = const.tile([P, STEPS_PER_BATCH, TILES, PAIRS], F32)
+        nc.vector.tensor_scalar_add(cos_table[:].rearrange("p r j i -> p (r j i)"), minus_two_squares[:], 1.0)
         for r in range(1, STEPS + 4):
             pipeline_round(r)

@@ -46,6 +46,8 @@ def tile_multilatentattention_pb_t_kernel(
         x_rows = x.flatten_outer_dims().rearrange("(s p j) e -> p s j e", p=P, j=TILES)
         wa_words = const.tile([P, X_PASSES, CKV * PACK], U8, align_bytes=64)
         wa_scales = const.tile([P, X_PASSES, CKV], U8, align_bytes=64)
+        wc_words = const.tile([P, X_PASSES, PACK, P * PACK], U8, align_bytes=64)
+        wc_scales = const.tile([P, X_PASSES, PACK, P], U8, align_bytes=64)
         wb_words = const.tile([P, KVR * PACK], U8, align_bytes=64)
         wb_scales = const.tile([P, KVR], U8, align_bytes=64)
 
@@ -78,7 +80,7 @@ def tile_multilatentattention_pb_t_kernel(
         for s in range(2, STEPS):
             load_x(s)
 
-        x_sorted, x_codes, x_scales, pe_sums, c_rounded = {}, {}, {}, {}, {}
+        x_sorted, x_codes, x_scales, pe_sums = {}, {}, {}, {}
         c_grouped, c_codes, c_scales, kv_sums, kf_rows = {}, {}, {}, {}, {}
 
         def sort_x(s):
@@ -118,31 +120,33 @@ def tile_multilatentattention_pb_t_kernel(
                     stop=(g == X_PASSES - 1),
                 )
 
+        def permute_wkva():
+            nc.vector.tensor_copy(
+                out=wc_words[:].bitcast(I32),
+                in_=wa_words[:, :, 0 : KVR * PACK].bitcast(I32).rearrange("p g (m t) -> p g t m", t=PACK),
+            )
+            for t in range(PACK):
+                nc.vector.tensor_copy(out=wc_scales[:, :, t, :], in_=wa_scales[:, :, t:KVR:PACK])
+
         def compress(s):
-            c_rounded[s] = work.tile([P, TILES, 2, P, 2], BF16, name="c_rounded")
+            c_grouped[s] = work.tile([P, TILES, P, PACK], BF16, name="c_grouped", align_bytes=64)
             for j in range(TILES):
-                c_sums = psum.tile([P, KVR], F32, name="c_sums", bufs=2)
-                x_times_wkva(s, j, 0, KVR, c_sums[:])
-                nc.scalar.copy(
-                    out=c_rounded[s][:, j], in_=c_sums[:].rearrange("p (q u e) -> p u q e", u=2, e=2)
-                )
+                c_flipped = psum.tile([P, PACK, P], F32, name="c_flipped", bufs=2)
+                for t in range(PACK):
+                    for g in range(X_PASSES):
+                        nc.tensor.matmul_mx(
+                            out=c_flipped[:, t, :],
+                            lhsT=wc_words[:, g, t, :].bitcast(FP8X4),
+                            lhsT_scale=wc_scales[:, g, t, :],
+                            rhs=x_codes[s][:, j, g, :].bitcast(FP8X4),
+                            rhs_scale=x_scales[s][:, j, g, :],
+                            start=(g == 0),
+                            stop=(g == X_PASSES - 1),
+                        )
+                nc.scalar.copy(out=c_grouped[s][:, j], in_=c_flipped[:].rearrange("p t n -> p n t"))
             pe_sums[s] = psum.tile([P, TILES, ROPE], F32, name="pe_sums")
             for j in range(TILES):
                 x_times_wkva(s, j, KVR, ROPE, pe_sums[s][:, j, :])
-
-        def transpose_c(s):
-            flipped = psum.tile([P, TILES, 2, P], F32, name="c_flipped")
-            for j in range(TILES):
-                for u in range(2):
-                    nc.tensor.transpose(
-                        flipped[:, j, u, :],
-                        c_rounded[s][:, j, u].rearrange("p q e -> p (q e)").bitcast(F32),
-                        identity[:],
-                    )
-            c_grouped[s] = work.tile([P, TILES, P, PACK], BF16, name="c_grouped", align_bytes=64)
-            nc.scalar.copy(
-                out=c_grouped[s][:].bitcast(F32), in_=flipped[:].rearrange("p j u t -> p j t u")
-            )
 
         def quantise_c(s):
             c_codes[s] = work.tile([P, TILES, P], U32, name="c_codes", align_bytes=64)
@@ -256,20 +260,21 @@ def tile_multilatentattention_pb_t_kernel(
         def pipeline_round(r):
             run(sort_x, r + 1)
             run(rotate, r - 2)
-            run(quantise_c, r - 3)
-            run(store, r - 4)
+            run(quantise_c, r - 2)
+            run(store, r - 3)
             run(quantise_x, r)
-            run(transpose_c, r - 2)
             run(compress, r - 1)
-            run(expand, r - 3)
+            run(expand, r - 2)
 
         sort_x(0)
-        pipeline_round(0)
+        sort_x(1)
+        permute_wkva()
+        quantise_x(0)
         minus_two_squares = const.tile([P, TABLE], F32)
         nc.vector.scalar_tensor_tensor(
             out=minus_two_squares[:], in0=sin_half[:], scalar=-2.0, in1=sin_half[:], op0=ALU.mult, op1=ALU.mult
         )
         cos_table = const.tile([P, STEPS_PER_BATCH, TILES, PAIRS], F32)
         nc.vector.tensor_scalar_add(cos_table[:].rearrange("p r j i -> p (r j i)"), minus_two_squares[:], 1.0)
-        for r in range(1, STEPS + 4):
+        for r in range(1, STEPS + 3):
             pipeline_round(r)

@@ -82,6 +82,7 @@ def tile_multilatentattention_pb_t_kernel(
 
         x_sorted, x_codes, x_scales, pe_sums = {}, {}, {}, {}
         c_grouped, c_codes, c_scales, kv_sums, kf_rows = {}, {}, {}, {}, {}
+        with_cos, with_sin, rows = {}, {}, {}
 
         def sort_x(s):
             x_sorted[s] = work.tile([P, TILES, X_PASSES, 2, P], F32, name="x_sorted")
@@ -96,7 +97,11 @@ def tile_multilatentattention_pb_t_kernel(
                 flipped = psum.tile([P, X_PASSES, 2, P], F32, name="x_flipped", bufs=2)
                 for g in range(X_PASSES):
                     for u in range(2):
-                        nc.tensor.transpose(flipped[:, g, u, :], x_sorted[s][:, j, g, u, :], identity[:])
+                        if s in x_sorted:
+                            words = x_sorted[s][:, j, g, u, :]
+                        else:
+                            words = x_all[:, s, j].bitcast(F32)[:, 2 * P * g + u : 2 * P * (g + 1) : 2]
+                        nc.tensor.transpose(flipped[:, g, u, :], words, identity[:])
                 nc.scalar.copy(
                     out=grouped[:, j].bitcast(F32), in_=flipped[:].rearrange("p g u t -> p g t u")
                 )
@@ -144,7 +149,7 @@ def tile_multilatentattention_pb_t_kernel(
                             stop=(g == X_PASSES - 1),
                         )
                 nc.scalar.copy(out=c_grouped[s][:, j], in_=c_flipped[:].rearrange("p t n -> p n t"))
-            pe_sums[s] = psum.tile([P, TILES, ROPE], F32, name="pe_sums")
+            pe_sums[s] = psum.tile([P, 2 * TILES, ROPE], F32, name="pe_sums")
             for j in range(TILES):
                 x_times_wkva(s, j, KVR, ROPE, pe_sums[s][:, j, :])
 
@@ -157,24 +162,24 @@ def tile_multilatentattention_pb_t_kernel(
                 in_=c_grouped[s][:].rearrange("p j t k -> p (j t k)"),
             )
 
-        def rotate(s):
-            pe = pe_sums[s][:].rearrange("p j (i e) -> p j e i", e=2)
+        def rotation_products(s):
+            pe = pe_sums[s][:, 0:TILES].rearrange("p j (i e) -> p j e i", e=2)
             cos = cos_table[:, s % STEPS_PER_BATCH]
             sin = sin_table[:, s % STEPS_PER_BATCH]
-            with_cos = work.tile([P, TILES, 2, PAIRS], F32, name="with_cos")
-            with_sin = work.tile([P, TILES, 2, PAIRS], F32, name="with_sin")
+            with_cos[s] = work.tile([P, TILES, 2, PAIRS], F32, name="with_cos")
+            with_sin[s] = work.tile([P, TILES, 2, PAIRS], F32, name="with_sin")
             nc.vector.tensor_tensor(
-                out=with_cos[:], in0=pe, in1=cos.unsqueeze(2).to_broadcast([P, TILES, 2, PAIRS]), op=ALU.mult
+                out=with_cos[s][:], in0=pe, in1=cos.unsqueeze(2).to_broadcast([P, TILES, 2, PAIRS]), op=ALU.mult
             )
-            nc.vector.scalar_tensor_tensor(
-                out=with_sin[:, :, 0, :], in0=pe[:, :, 1, :], scalar=-1.0, in1=sin, op0=ALU.mult, op1=ALU.mult
-            )
-            nc.vector.tensor_tensor(out=with_sin[:, :, 1, :], in0=pe[:, :, 0, :], in1=sin, op=ALU.mult)
-            kf_rows[s] = result.tile([P, H, TILES, KF], F32, name="kf_rows")
+            nc.vector.tensor_tensor(out=with_sin[s][:], in0=pe[:, :, ::-1, :], in1=sin, op=ALU.mult)
+
+        def rotation_sum(s):
+            rows[s] = result.tile([P, H, TILES * (KF + VDIM)], F32, name="rows")
+            kf_rows[s] = rows[s][:, :, 0 : TILES * KF].rearrange("p h (j d) -> p h j d", j=TILES)
             nc.gpsimd.tensor_tensor(
                 out=kf_rows[s][:, 0, :, NOPE:KF].rearrange("p j (i e) -> p j i e", e=2),
-                in0=with_cos[:].rearrange("p j e i -> p j i e"),
-                in1=with_sin[:].rearrange("p j e i -> p j i e"),
+                in0=with_cos[s][:].rearrange("p j e i -> p j i e"),
+                in1=with_sin[s][:].rearrange("p j e i -> p j i e"),
                 op=ALU.add,
             )
             nc.gpsimd.tensor_scalar(
@@ -186,33 +191,46 @@ def tile_multilatentattention_pb_t_kernel(
                 op1=ALU.add,
             )
 
+        def c_times_wkvb(s, j, first, width, sums):
+            nc.tensor.matmul_mx(
+                out=sums,
+                lhsT=c_codes[s][:, j, :].bitcast(FP8X4),
+                lhsT_scale=c_scales[s][:, j, :],
+                rhs=wb_words[:, PACK * first : PACK * (first + width)].bitcast(FP8X4),
+                rhs_scale=wb_scales[:, first : first + width],
+                start=True,
+                stop=True,
+            )
+
         def expand(s):
-            for j in range(TILES):
-                kv_sums[s, j] = psum.tile([P, H, 2, NOPE], F32, name="kv_sums", bufs=2)
-                nc.tensor.matmul_mx(
-                    out=kv_sums[s, j][:].rearrange("p h c d -> p (h c d)"),
-                    lhsT=c_codes[s][:, j, :].bitcast(FP8X4),
-                    lhsT_scale=c_scales[s][:, j, :],
-                    rhs=wb_words[:].bitcast(FP8X4),
-                    rhs_scale=wb_scales[:],
-                    start=True,
-                    stop=True,
-                )
+            kv_sums[s, 0] = psum.tile([P, KVR], F32, name="kv_tile0")
+            kv_sums[s, 1] = psum.tile([P, KVR], F32, name="kv_tile1_front")
+            kv_sums[s, 2] = psum.tile([P, KVR], F32, name="kv_tile1_back")
+            c_times_wkvb(s, 0, 0, KVR, kv_sums[s, 0][:])
+            c_times_wkvb(s, 1, 0, KVR // 2, kv_sums[s, 1][:, 0 : KVR // 2])
+            c_times_wkvb(s, 1, KVR // 2, KVR // 2, kv_sums[s, 2][:, 0 : KVR // 2])
 
         def store(s):
-            v_rows = result.tile([P, H, TILES, VDIM], F32, name="v_rows")
-            nc.scalar.copy(out=kf_rows[s][:, :, 0, 0:NOPE], in_=kv_sums[s, 0][:, :, 0, :])
-            nc.scalar.copy(out=v_rows[:, :, 0, :], in_=kv_sums[s, 0][:, :, 1, :])
-            nc.vector.tensor_copy(out=kf_rows[s][:, :, 1, 0:NOPE], in_=kv_sums[s, 1][:, :, 0, :])
-            nc.vector.tensor_copy(out=v_rows[:, :, 1, :], in_=kv_sums[s, 1][:, :, 1, :])
+            units = rows[s][:].rearrange("p h (u d) -> p h u d", d=NOPE)
+            tile0 = units[:, :, 0:7:6, :]
+            tile1 = units[:, :, 3:8:4, :]
+            nc.vector.tensor_copy(
+                out=tile1[:, H // 2 : H],
+                in_=kv_sums[s, 2][:, 0 : KVR // 2].rearrange("p (h c d) -> p h c d", c=2, d=NOPE),
+            )
+            nc.scalar.copy(out=tile0, in_=kv_sums[s, 0][:].rearrange("p (h c d) -> p h c d", c=2, d=NOPE))
+            nc.scalar.copy(
+                out=tile1[:, 0 : H // 2],
+                in_=kv_sums[s, 1][:, 0 : KVR // 2].rearrange("p (h c d) -> p h c d", c=2, d=NOPE),
+            )
             b, first = s // STEPS_PER_BATCH, STEP * (s % STEPS_PER_BATCH)
             nc.sync.dma_start(
                 out=kf[b, :, first : first + STEP, :].rearrange("h (p j) d -> p h (j d)", j=TILES),
-                in_=kf_rows[s][:].rearrange("p h j d -> p h (j d)"),
+                in_=rows[s][:, :, 0 : TILES * KF],
             )
             nc.sync.dma_start(
                 out=v[b, :, first : first + STEP, :].rearrange("h (p j) d -> p h (j d)", j=TILES),
-                in_=v_rows[:].rearrange("p h j d -> p h (j d)"),
+                in_=rows[s][:, :, TILES * KF : TILES * (KF + VDIM)],
             )
 
         TABLE = STEPS_PER_BATCH * TILES * PAIRS
@@ -246,10 +264,14 @@ def tile_multilatentattention_pb_t_kernel(
         nc.vector.tensor_tensor(
             out=part_turn[:], in0=turns[:].rearrange("p n i -> p (n i)"), in1=whole_turns[:], op=ALU.subtract
         )
-        sin_table = const.tile([P, STEPS_PER_BATCH, TILES, PAIRS], F32)
-        nc.scalar.activation(
-            out=sin_table[:].rearrange("p r j i -> p (r j i)"), in_=part_turn[:], func=ACT.Sin, scale=2.0 * math.pi
-        )
+        sin_table = const.tile([P, STEPS_PER_BATCH, TILES, 2, PAIRS], F32)
+        for e, sign in ((0, -1.0), (1, 1.0)):
+            nc.scalar.activation(
+                out=sin_table[:, :, :, e, :].rearrange("p r j i -> p (r j) i"),
+                in_=part_turn[:].rearrange("p (n i) -> p n i", i=PAIRS),
+                func=ACT.Sin,
+                scale=sign * 2.0 * math.pi,
+            )
         sin_half = const.tile([P, TABLE], F32)
         nc.scalar.activation(out=sin_half[:], in_=part_turn[:], func=ACT.Sin, scale=math.pi)
 
@@ -259,14 +281,14 @@ def tile_multilatentattention_pb_t_kernel(
 
         def pipeline_round(r):
             run(sort_x, r + 1)
-            run(rotate, r - 2)
+            run(rotation_products, r - 2)
+            run(rotation_sum, r - 2)
             run(quantise_c, r - 2)
             run(store, r - 3)
             run(quantise_x, r)
             run(compress, r - 1)
             run(expand, r - 2)
 
-        sort_x(0)
         sort_x(1)
         permute_wkva()
         quantise_x(0)

@@ -85,10 +85,10 @@ def tile_multilatentattention_pb_t_kernel(
         with_cos, with_sin, rows = {}, {}, {}
 
         def sort_x(s):
-            x_sorted[s] = work.tile([P, TILES, X_PASSES, 2, P], F32, name="x_sorted")
+            x_sorted[s] = work.tile([P, X_PASSES, 2, P], F32, name="x_sorted")
             nc.vector.tensor_copy(
                 out=x_sorted[s][:],
-                in_=x_all[:, s].bitcast(F32).rearrange("p j (g q u) -> p j g u q", g=X_PASSES, u=2),
+                in_=x_all[:, s, 0].bitcast(F32).rearrange("p (g q u) -> p g u q", g=X_PASSES, u=2),
             )
 
         def quantise_x(s):
@@ -97,8 +97,8 @@ def tile_multilatentattention_pb_t_kernel(
                 flipped = psum.tile([P, X_PASSES, 2, P], F32, name="x_flipped", bufs=2)
                 for g in range(X_PASSES):
                     for u in range(2):
-                        if s in x_sorted:
-                            words = x_sorted[s][:, j, g, u, :]
+                        if j == 0 and s in x_sorted:
+                            words = x_sorted[s][:, g, u, :]
                         else:
                             words = x_all[:, s, j].bitcast(F32)[:, 2 * P * g + u : 2 * P * (g + 1) : 2]
                         nc.tensor.transpose(flipped[:, g, u, :], words, identity[:])
@@ -176,19 +176,17 @@ def tile_multilatentattention_pb_t_kernel(
         def rotation_sum(s):
             rows[s] = result.tile([P, H, TILES * (KF + VDIM)], F32, name="rows")
             kf_rows[s] = rows[s][:, :, 0 : TILES * KF].rearrange("p h (j d) -> p h j d", j=TILES)
-            nc.gpsimd.tensor_tensor(
+            nc.vector.tensor_tensor(
                 out=kf_rows[s][:, 0, :, NOPE:KF].rearrange("p j (i e) -> p j i e", e=2),
                 in0=with_cos[s][:].rearrange("p j e i -> p j i e"),
                 in1=with_sin[s][:].rearrange("p j e i -> p j i e"),
                 op=ALU.add,
             )
-            nc.gpsimd.tensor_scalar(
+
+        def repeat_for_heads(s):
+            nc.vector.tensor_copy(
                 out=kf_rows[s][:, 1:H, :, NOPE:KF],
-                in0=kf_rows[s][:, 0:1, :, NOPE:KF].to_broadcast([P, H - 1, TILES, ROPE]),
-                scalar1=1.0,
-                scalar2=0.0,
-                op0=ALU.mult,
-                op1=ALU.add,
+                in_=kf_rows[s][:, 0:1, :, NOPE:KF].to_broadcast([P, H - 1, TILES, ROPE]),
             )
 
         def c_times_wkvb(s, j, first, width, sums):
@@ -280,10 +278,11 @@ def tile_multilatentattention_pb_t_kernel(
                 stage(s)
 
         def pipeline_round(r):
-            run(sort_x, r + 1)
             run(rotation_products, r - 2)
+            run(sort_x, r + 1)
             run(rotation_sum, r - 2)
             run(quantise_c, r - 2)
+            run(repeat_for_heads, r - 2)
             run(store, r - 3)
             run(quantise_x, r)
             run(compress, r - 1)

@@ -24,6 +24,10 @@ TILES = 2
 STEP = P * TILES
 STEPS = B * N // STEP
 STEPS_PER_BATCH = N // STEP
+GROUP = 2
+GROUPS = STEPS // GROUP
+GROUPS_PER_BATCH = STEPS_PER_BATCH // GROUP
+ROWS = GROUP * TILES
 BASE = 10000.0
 
 FLOPS = 2 * B * N * (E * CKV + KVR * H * (NOPE + VDIM))
@@ -38,12 +42,12 @@ def tile_multilatentattention_pb_t_kernel(
     with (
         tc.tile_pool(name="const", bufs=1) as const,
         tc.tile_pool(name="work", bufs=2) as work,
-        tc.tile_pool(name="result", bufs=5) as result,
+        tc.tile_pool(name="result", bufs=4) as result,
         tc.psum_pool(name="psum", bufs=1) as psum,
         tc.manual_schedule(),
     ):
         x_all = const.tile([P, STEPS, TILES, E], BF16)
-        x_rows = x.flatten_outer_dims().rearrange("(s p j) e -> p s j e", p=P, j=TILES)
+        x_rows = x.flatten_outer_dims().rearrange("(q p a j) e -> p q a j e", p=P, a=GROUP, j=TILES)
         wa_words = const.tile([P, X_PASSES, CKV * PACK], U8, align_bytes=64)
         wa_scales = const.tile([P, X_PASSES, CKV], U8, align_bytes=64)
         wc_words = const.tile([P, X_PASSES, PACK, P * PACK], U8, align_bytes=64)
@@ -55,7 +59,7 @@ def tile_multilatentattention_pb_t_kernel(
         nc.vector.memset(wb_scales[:].bitcast(I32), 0)
 
         def load_x(s):
-            nc.sync.dma_start(out=x_all[:, s], in_=x_rows[:, s])
+            nc.sync.dma_start(out=x_all[:, s], in_=x_rows[:, s // GROUP, s % GROUP])
 
         load_x(0)
         load_x(1)
@@ -173,9 +177,19 @@ def tile_multilatentattention_pb_t_kernel(
             )
             nc.vector.tensor_tensor(out=with_sin[s][:], in0=pe[:, :, ::-1, :], in1=sin, op=ALU.mult)
 
+        def stored_together(s):
+            if s // GROUP < GROUPS - 1:
+                return GROUP * (s // GROUP), GROUP
+            return s, 1
+
         def rotation_sum(s):
-            rows[s] = result.tile([P, H, TILES * (KF + VDIM)], F32, name="rows")
-            kf_rows[s] = rows[s][:, :, 0 : TILES * KF].rearrange("p h (j d) -> p h j d", j=TILES)
+            first_step, steps = stored_together(s)
+            if s == first_step:
+                rows[first_step] = result.tile([P, H, steps * TILES * (KF + VDIM)], F32, name="rows")
+            token = TILES * (s - first_step)
+            kf_rows[s] = rows[first_step][:, :, KF * token : KF * (token + TILES)].rearrange(
+                "p h (j d) -> p h j d", j=TILES
+            )
             nc.vector.tensor_tensor(
                 out=kf_rows[s][:, 0, :, NOPE:KF].rearrange("p j (i e) -> p j i e", e=2),
                 in0=with_cos[s][:].rearrange("p j e i -> p j i e"),
@@ -209,9 +223,12 @@ def tile_multilatentattention_pb_t_kernel(
             c_times_wkvb(s, 1, KVR // 2, KVR // 2, kv_sums[s, 2][:, 0 : KVR // 2])
 
         def store(s):
-            units = rows[s][:].rearrange("p h (u d) -> p h u d", d=NOPE)
-            tile0 = units[:, :, 0:7:6, :]
-            tile1 = units[:, :, 3:8:4, :]
+            first_step, steps = stored_together(s)
+            n = steps * TILES
+            units = rows[first_step][:].rearrange("p h (u d) -> p h u d", d=NOPE)
+            m = TILES * (s - first_step)
+            tile0 = units[:, :, 3 * m : 3 * n + m + 1 : 3 * n - 2 * m, :]
+            tile1 = units[:, :, 3 * (m + 1) : 3 * n + m + 2 : 3 * n - 2 * (m + 1), :]
             nc.vector.tensor_copy(
                 out=tile1[:, H // 2 : H],
                 in_=kv_sums[s, 2][:, 0 : KVR // 2].rearrange("p (h c d) -> p h c d", c=2, d=NOPE),
@@ -221,20 +238,22 @@ def tile_multilatentattention_pb_t_kernel(
                 out=tile1[:, 0 : H // 2],
                 in_=kv_sums[s, 1][:, 0 : KVR // 2].rearrange("p (h c d) -> p h c d", c=2, d=NOPE),
             )
-            b, first = s // STEPS_PER_BATCH, STEP * (s % STEPS_PER_BATCH)
-            nc.sync.dma_start(
-                out=kf[b, :, first : first + STEP, :].rearrange("h (p j) d -> p h (j d)", j=TILES),
-                in_=rows[s][:, :, 0 : TILES * KF],
-            )
-            nc.sync.dma_start(
-                out=v[b, :, first : first + STEP, :].rearrange("h (p j) d -> p h (j d)", j=TILES),
-                in_=rows[s][:, :, TILES * KF : TILES * (KF + VDIM)],
-            )
+            if s == first_step + steps - 1:
+                q = s // GROUP
+                b, first = q // GROUPS_PER_BATCH, GROUP * STEP * (q % GROUPS_PER_BATCH)
+                skipped = TILES * (first_step % GROUP)
+                for out, start, width in ((kf, 0, KF), (v, n * KF, VDIM)):
+                    nc.sync.dma_start(
+                        out=out[b, :, first : first + GROUP * STEP, :].rearrange("h (p t) d -> p h (t d)", t=ROWS)[
+                            :, :, width * skipped : width * (skipped + n)
+                        ],
+                        in_=rows[first_step][:, :, start : start + n * width],
+                    )
 
         TABLE = STEPS_PER_BATCH * TILES * PAIRS
         position_int = const.tile([P, STEPS_PER_BATCH * TILES], I32)
         nc.gpsimd.iota(
-            position_int[:], pattern=[[STEP, STEPS_PER_BATCH], [1, TILES]], base=0, channel_multiplier=TILES
+            position_int[:], pattern=[[GROUP * STEP, GROUPS_PER_BATCH], [1, ROWS]], base=0, channel_multiplier=ROWS
         )
         identity = const.tile([P, P], F32)
         make_identity(nc, identity[:])
@@ -278,12 +297,12 @@ def tile_multilatentattention_pb_t_kernel(
                 stage(s)
 
         def pipeline_round(r):
+            run(store, r - 3)
             run(rotation_products, r - 2)
             run(sort_x, r + 1)
             run(rotation_sum, r - 2)
             run(quantise_c, r - 2)
             run(repeat_for_heads, r - 2)
-            run(store, r - 3)
             run(quantise_x, r)
             run(compress, r - 1)
             run(expand, r - 2)

@@ -84,16 +84,9 @@ def tile_multilatentattention_pb_t_kernel(
         for s in range(2, STEPS):
             load_x(s)
 
-        x_sorted, x_codes, x_scales, pe_sums = {}, {}, {}, {}
+        x_codes, x_scales, pe_sums = {}, {}, {}
         c_grouped, c_codes, c_scales, kv_sums, kf_rows = {}, {}, {}, {}, {}
         with_cos, with_sin, rows = {}, {}, {}
-
-        def sort_x(s):
-            x_sorted[s] = work.tile([P, X_PASSES, 2, P], F32, name="x_sorted")
-            nc.vector.tensor_copy(
-                out=x_sorted[s][:],
-                in_=x_all[:, s, 0].bitcast(F32).rearrange("p (g q u) -> p g u q", g=X_PASSES, u=2),
-            )
 
         def quantise_x(s):
             grouped = work.tile([P, TILES, X_PASSES, P, PACK], BF16, name="x_grouped", align_bytes=64)
@@ -101,10 +94,7 @@ def tile_multilatentattention_pb_t_kernel(
                 flipped = psum.tile([P, X_PASSES, 2, P], F32, name="x_flipped", bufs=2)
                 for g in range(X_PASSES):
                     for u in range(2):
-                        if j == 0 and s in x_sorted:
-                            words = x_sorted[s][:, g, u, :]
-                        else:
-                            words = x_all[:, s, j].bitcast(F32)[:, 2 * P * g + u : 2 * P * (g + 1) : 2]
+                        words = x_all[:, s, j].bitcast(F32)[:, 2 * P * g + u : 2 * P * (g + 1) : 2]
                         nc.tensor.transpose(flipped[:, g, u, :], words, identity[:])
                 nc.scalar.copy(
                     out=grouped[:, j].bitcast(F32), in_=flipped[:].rearrange("p g u t -> p g t u")
@@ -299,7 +289,6 @@ def tile_multilatentattention_pb_t_kernel(
         def pipeline_round(r):
             run(store, r - 3)
             run(rotation_products, r - 2)
-            run(sort_x, r + 1)
             run(rotation_sum, r - 2)
             run(quantise_c, r - 2)
             run(repeat_for_heads, r - 2)
@@ -307,7 +296,6 @@ def tile_multilatentattention_pb_t_kernel(
             run(compress, r - 1)
             run(expand, r - 2)
 
-        sort_x(1)
         permute_wkva()
         quantise_x(0)
         minus_two_squares = const.tile([P, TABLE], F32)

@@ -27,6 +27,7 @@ STEPS_PER_BATCH = N // STEP
 GROUP = 2
 GROUPS = STEPS // GROUP
 GROUPS_PER_BATCH = STEPS_PER_BATCH // GROUP
+SINGLE_GROUPS = 2
 ROWS = GROUP * TILES
 BASE = 10000.0
 
@@ -55,6 +56,11 @@ def tile_multilatentattention_pb_t_kernel(
         wb_words = const.tile([P, KVR * PACK], U8, align_bytes=64)
         wb_scales = const.tile([P, KVR], U8, align_bytes=64)
 
+        zero = const.tile([P, 1], F32)
+        nc.vector.memset(zero[:], 0.0)
+        sin_of_zero = const.tile([P, 1], F32)
+        nc.scalar.activation(out=sin_of_zero[:], in_=zero[:], func=ACT.Sin)
+
         nc.vector.memset(wa_scales[:].rearrange("p g n -> p (g n)").bitcast(I32), 0)
         nc.vector.memset(wb_scales[:].bitcast(I32), 0)
 
@@ -62,7 +68,6 @@ def tile_multilatentattention_pb_t_kernel(
             nc.sync.dma_start(out=x_all[:, s], in_=x_rows[:, s // GROUP, s % GROUP])
 
         load_x(0)
-        load_x(1)
         for quad in range(4):
             nc.sync.dma_start(
                 out=wa_scales[32 * quad : 32 * quad + 4].bitcast(I32),
@@ -72,6 +77,7 @@ def tile_multilatentattention_pb_t_kernel(
             out=wa_words[:].bitcast(I32),
             in_=Wkva_words.rearrange("g p n t -> p g (n t)").bitcast(I32),
         )
+        load_x(1)
         for quad in range(4):
             nc.sync.dma_start(
                 out=wb_scales[32 * quad : 32 * quad + 4].bitcast(I32),
@@ -121,11 +127,12 @@ def tile_multilatentattention_pb_t_kernel(
 
         def permute_wkva():
             nc.vector.tensor_copy(
+                out=wc_scales[:], in_=wa_scales[:, :, 0:KVR].rearrange("p g (m t) -> p g t m", t=PACK)
+            )
+            nc.vector.tensor_copy(
                 out=wc_words[:].bitcast(I32),
                 in_=wa_words[:, :, 0 : KVR * PACK].bitcast(I32).rearrange("p g (m t) -> p g t m", t=PACK),
             )
-            for t in range(PACK):
-                nc.vector.tensor_copy(out=wc_scales[:, :, t, :], in_=wa_scales[:, :, t:KVR:PACK])
 
         def compress(s):
             c_grouped[s] = work.tile([P, TILES, P, PACK], BF16, name="c_grouped", align_bytes=64)
@@ -168,7 +175,7 @@ def tile_multilatentattention_pb_t_kernel(
             nc.vector.tensor_tensor(out=with_sin[s][:], in0=pe[:, :, ::-1, :], in1=sin, op=ALU.mult)
 
         def stored_together(s):
-            if s // GROUP < GROUPS - 1:
+            if s // GROUP < GROUPS - SINGLE_GROUPS:
                 return GROUP * (s // GROUP), GROUP
             return s, 1
 
@@ -206,11 +213,9 @@ def tile_multilatentattention_pb_t_kernel(
 
         def expand(s):
             kv_sums[s, 0] = psum.tile([P, KVR], F32, name="kv_tile0")
-            kv_sums[s, 1] = psum.tile([P, KVR], F32, name="kv_tile1_front")
-            kv_sums[s, 2] = psum.tile([P, KVR], F32, name="kv_tile1_back")
+            kv_sums[s, 1] = psum.tile([P, KVR], F32, name="kv_tile1")
             c_times_wkvb(s, 0, 0, KVR, kv_sums[s, 0][:])
-            c_times_wkvb(s, 1, 0, KVR // 2, kv_sums[s, 1][:, 0 : KVR // 2])
-            c_times_wkvb(s, 1, KVR // 2, KVR // 2, kv_sums[s, 2][:, 0 : KVR // 2])
+            c_times_wkvb(s, 1, 0, KVR, kv_sums[s, 1][:])
 
         def store(s):
             first_step, steps = stored_together(s)
@@ -219,15 +224,9 @@ def tile_multilatentattention_pb_t_kernel(
             m = TILES * (s - first_step)
             tile0 = units[:, :, 3 * m : 3 * n + m + 1 : 3 * n - 2 * m, :]
             tile1 = units[:, :, 3 * (m + 1) : 3 * n + m + 2 : 3 * n - 2 * (m + 1), :]
-            nc.vector.tensor_copy(
-                out=tile1[:, H // 2 : H],
-                in_=kv_sums[s, 2][:, 0 : KVR // 2].rearrange("p (h c d) -> p h c d", c=2, d=NOPE),
-            )
+            copy_tile1 = nc.scalar.copy if s >= STEPS - 3 else nc.vector.tensor_copy
             nc.scalar.copy(out=tile0, in_=kv_sums[s, 0][:].rearrange("p (h c d) -> p h c d", c=2, d=NOPE))
-            nc.scalar.copy(
-                out=tile1[:, 0 : H // 2],
-                in_=kv_sums[s, 1][:, 0 : KVR // 2].rearrange("p (h c d) -> p h c d", c=2, d=NOPE),
-            )
+            copy_tile1(out=tile1, in_=kv_sums[s, 1][:].rearrange("p (h c d) -> p h c d", c=2, d=NOPE))
             if s == first_step + steps - 1:
                 q = s // GROUP
                 b, first = q // GROUPS_PER_BATCH, GROUP * STEP * (q % GROUPS_PER_BATCH)
@@ -248,13 +247,11 @@ def tile_multilatentattention_pb_t_kernel(
         identity = const.tile([P, P], F32)
         make_identity(nc, identity[:])
 
-        position = const.tile([P, STEPS_PER_BATCH * TILES], F32)
-        nc.vector.tensor_copy(out=position[:], in_=position_int[:])
-
         ratio = BASE ** (-2.0 / ROPE)
         turns = const.tile([P, STEPS_PER_BATCH * TILES, PAIRS], F32)
-        nc.vector.tensor_scalar_mul(turns[:, :, 0], position[:], 0.5 / math.pi)
-        width = 1
+        width = 8
+        for i in range(width):
+            nc.vector.tensor_scalar_mul(turns[:, :, i], position_int[:], ratio**i * 0.5 / math.pi)
         while width < PAIRS:
             nc.vector.tensor_scalar_mul(turns[:, :, width : 2 * width], turns[:, :, 0:width], ratio**width)
             width *= 2
@@ -271,6 +268,25 @@ def tile_multilatentattention_pb_t_kernel(
         nc.vector.tensor_tensor(
             out=part_turn[:], in0=turns[:].rearrange("p n i -> p (n i)"), in1=whole_turns[:], op=ALU.subtract
         )
+        def run(stage, s):
+            if 0 <= s < STEPS:
+                stage(s)
+
+        def pipeline_round(r):
+            if r >= STEPS:
+                run(quantise_c, r - 2)
+            run(store, r - 3)
+            run(rotation_products, r - 2)
+            if r < STEPS:
+                run(quantise_c, r - 2)
+            run(rotation_sum, r - 2)
+            run(quantise_x, r)
+            run(repeat_for_heads, r - 2)
+            run(compress, r - 1)
+            run(expand, r - 2)
+
+        permute_wkva()
+        quantise_x(0)
         sin_table = const.tile([P, STEPS_PER_BATCH, TILES, 2, PAIRS], F32)
         for e, sign in ((0, -1.0), (1, 1.0)):
             nc.scalar.activation(
@@ -282,22 +298,6 @@ def tile_multilatentattention_pb_t_kernel(
         sin_half = const.tile([P, TABLE], F32)
         nc.scalar.activation(out=sin_half[:], in_=part_turn[:], func=ACT.Sin, scale=math.pi)
 
-        def run(stage, s):
-            if 0 <= s < STEPS:
-                stage(s)
-
-        def pipeline_round(r):
-            run(store, r - 3)
-            run(rotation_products, r - 2)
-            run(rotation_sum, r - 2)
-            run(quantise_c, r - 2)
-            run(repeat_for_heads, r - 2)
-            run(quantise_x, r)
-            run(compress, r - 1)
-            run(expand, r - 2)
-
-        permute_wkva()
-        quantise_x(0)
         minus_two_squares = const.tile([P, TABLE], F32)
         nc.vector.scalar_tensor_tensor(
             out=minus_two_squares[:], in0=sin_half[:], scalar=-2.0, in1=sin_half[:], op0=ALU.mult, op1=ALU.mult

@@ -27,7 +27,7 @@ STEPS_PER_BATCH = N // STEP
 GROUP = 2
 GROUPS = STEPS // GROUP
 GROUPS_PER_BATCH = STEPS_PER_BATCH // GROUP
-SINGLE_GROUPS = 2
+SINGLE_GROUPS = 4
 ROWS = GROUP * TILES
 BASE = 10000.0
 
@@ -67,17 +67,25 @@ def tile_multilatentattention_pb_t_kernel(
         def load_x(s):
             nc.sync.dma_start(out=x_all[:, s], in_=x_rows[:, s // GROUP, s % GROUP])
 
-        load_x(0)
+        def load_x_tile(s, j):
+            nc.sync.dma_start(out=x_all[:, s, j], in_=x_rows[:, s // GROUP, s % GROUP, j])
+
+        def load_wkva(first, last):
+            nc.sync.dma_start(
+                out=wa_words[:, :, PACK * first : PACK * last].bitcast(I32),
+                in_=Wkva_words[:, :, first:last, :].rearrange("g p n t -> p g (n t)").bitcast(I32),
+            )
+
+        load_x_tile(0, 0)
+        load_x_tile(0, 1)
         for quad in range(4):
             nc.sync.dma_start(
                 out=wa_scales[32 * quad : 32 * quad + 4].bitcast(I32),
                 in_=Wkva_scales[:, 4 * quad : 4 * quad + 4, :].rearrange("g r n -> r g n").bitcast(I32),
             )
-        nc.sync.dma_start(
-            out=wa_words[:].bitcast(I32),
-            in_=Wkva_words.rearrange("g p n t -> p g (n t)").bitcast(I32),
-        )
         load_x(1)
+        load_wkva(0, KVR)
+        load_wkva(KVR, CKV)
         for quad in range(4):
             nc.sync.dma_start(
                 out=wb_scales[32 * quad : 32 * quad + 4].bitcast(I32),
@@ -90,12 +98,12 @@ def tile_multilatentattention_pb_t_kernel(
         for s in range(2, STEPS):
             load_x(s)
 
-        x_codes, x_scales, pe_sums = {}, {}, {}
+        x_grouped, x_codes, x_scales, pe_sums = {}, {}, {}, {}
         c_grouped, c_codes, c_scales, kv_sums, kf_rows = {}, {}, {}, {}, {}
         with_cos, with_sin, rows = {}, {}, {}
 
-        def quantise_x(s):
-            grouped = work.tile([P, TILES, X_PASSES, P, PACK], BF16, name="x_grouped", align_bytes=64)
+        def flip_x(s):
+            x_grouped[s] = work.tile([P, TILES, X_PASSES, P, PACK], BF16, name="x_grouped", align_bytes=64)
             for j in range(TILES):
                 flipped = psum.tile([P, X_PASSES, 2, P], F32, name="x_flipped", bufs=2)
                 for g in range(X_PASSES):
@@ -103,15 +111,18 @@ def tile_multilatentattention_pb_t_kernel(
                         words = x_all[:, s, j].bitcast(F32)[:, 2 * P * g + u : 2 * P * (g + 1) : 2]
                         nc.tensor.transpose(flipped[:, g, u, :], words, identity[:])
                 nc.scalar.copy(
-                    out=grouped[:, j].bitcast(F32), in_=flipped[:].rearrange("p g u t -> p g t u")
+                    out=x_grouped[s][:, j].bitcast(F32), in_=flipped[:].rearrange("p g u t -> p g t u")
                 )
+
+        def quantise_x(s):
             x_codes[s] = work.tile([P, TILES, X_PASSES, P], U32, name="x_codes", align_bytes=64)
             x_scales[s] = work.tile([P, TILES, X_PASSES, P], U8, name="x_scales", align_bytes=64)
-            nc.vector.quantize_mx(
-                out=x_codes[s][:].rearrange("p j g t -> p (j g t)").bitcast(FP8X4),
-                scales=x_scales[s][:].rearrange("p j g t -> p (j g t)"),
-                in_=grouped[:].rearrange("p j g t k -> p (j g t k)"),
-            )
+            for tiles in [slice(j, j + 1) for j in range(TILES)] if s == 0 else [slice(0, TILES)]:
+                nc.vector.quantize_mx(
+                    out=x_codes[s][:, tiles].rearrange("p j g t -> p (j g t)").bitcast(FP8X4),
+                    scales=x_scales[s][:, tiles].rearrange("p j g t -> p (j g t)"),
+                    in_=x_grouped[s][:, tiles].rearrange("p j g t k -> p (j g t k)"),
+                )
 
         def x_times_wkva(s, j, first, width, sums):
             for g in range(X_PASSES):
@@ -125,10 +136,12 @@ def tile_multilatentattention_pb_t_kernel(
                     stop=(g == X_PASSES - 1),
                 )
 
-        def permute_wkva():
+        def permute_scales():
             nc.vector.tensor_copy(
                 out=wc_scales[:], in_=wa_scales[:, :, 0:KVR].rearrange("p g (m t) -> p g t m", t=PACK)
             )
+
+        def permute_words():
             nc.vector.tensor_copy(
                 out=wc_words[:].bitcast(I32),
                 in_=wa_words[:, :, 0 : KVR * PACK].bitcast(I32).rearrange("p g (m t) -> p g t m", t=PACK),
@@ -150,7 +163,7 @@ def tile_multilatentattention_pb_t_kernel(
                             stop=(g == X_PASSES - 1),
                         )
                 nc.scalar.copy(out=c_grouped[s][:, j], in_=c_flipped[:].rearrange("p t n -> p n t"))
-            pe_sums[s] = psum.tile([P, 2 * TILES, ROPE], F32, name="pe_sums")
+            pe_sums[s] = psum.tile([P, 2 * TILES, ROPE], F32, name="pe_sums", bufs=2)
             for j in range(TILES):
                 x_times_wkva(s, j, KVR, ROPE, pe_sums[s][:, j, :])
 
@@ -280,13 +293,21 @@ def tile_multilatentattention_pb_t_kernel(
             if r < STEPS:
                 run(quantise_c, r - 2)
             run(rotation_sum, r - 2)
-            run(quantise_x, r)
+            if r > 1:
+                run(flip_x, r)
+                run(quantise_x, r)
             run(repeat_for_heads, r - 2)
             run(compress, r - 1)
             run(expand, r - 2)
 
-        permute_wkva()
+        permute_scales()
+        flip_x(0)
         quantise_x(0)
+        permute_words()
+        flip_x(1)
+        quantise_x(1)
+        sin_half = const.tile([P, TABLE], F32)
+        nc.scalar.activation(out=sin_half[:], in_=part_turn[:], func=ACT.Sin, scale=math.pi)
         sin_table = const.tile([P, STEPS_PER_BATCH, TILES, 2, PAIRS], F32)
         for e, sign in ((0, -1.0), (1, 1.0)):
             nc.scalar.activation(
@@ -295,9 +316,6 @@ def tile_multilatentattention_pb_t_kernel(
                 func=ACT.Sin,
                 scale=sign * 2.0 * math.pi,
             )
-        sin_half = const.tile([P, TABLE], F32)
-        nc.scalar.activation(out=sin_half[:], in_=part_turn[:], func=ACT.Sin, scale=math.pi)
-
         minus_two_squares = const.tile([P, TABLE], F32)
         nc.vector.scalar_tensor_tensor(
             out=minus_two_squares[:], in0=sin_half[:], scalar=-2.0, in1=sin_half[:], op0=ALU.mult, op1=ALU.mult

@@ -47,13 +47,13 @@ def tile_multilatentattention_pb_t_kernel(
         tc.psum_pool(name="psum", bufs=1) as psum,
         tc.manual_schedule(),
     ):
-        x_all = const.tile([P, STEPS, TILES, E], BF16)
+        x_all = const.tile([P, STEPS, TILES, E], BF16, align_bytes=256)
         x_rows = x.flatten_outer_dims().rearrange("(q p a j) e -> p q a j e", p=P, a=GROUP, j=TILES)
-        wa_words = const.tile([P, X_PASSES, CKV * PACK], U8, align_bytes=64)
+        wa_words = const.tile([P, X_PASSES, CKV * PACK], U8, align_bytes=256)
         wa_scales = const.tile([P, X_PASSES, CKV], U8, align_bytes=64)
         wc_words = const.tile([P, X_PASSES, PACK, P * PACK], U8, align_bytes=64)
         wc_scales = const.tile([P, X_PASSES, PACK, P], U8, align_bytes=64)
-        wb_words = const.tile([P, KVR * PACK], U8, align_bytes=64)
+        wb_words = const.tile([P, KVR * PACK], U8, align_bytes=256)
         wb_scales = const.tile([P, KVR], U8, align_bytes=64)
 
         zero = const.tile([P, 1], F32)
@@ -195,7 +195,9 @@ def tile_multilatentattention_pb_t_kernel(
         def rotation_sum(s):
             first_step, steps = stored_together(s)
             if s == first_step:
-                rows[first_step] = result.tile([P, H, steps * TILES * (KF + VDIM)], F32, name="rows")
+                rows[first_step] = result.tile(
+                    [P, H, steps * TILES * (KF + VDIM)], F32, name="rows", align_bytes=256
+                )
             token = TILES * (s - first_step)
             kf_rows[s] = rows[first_step][:, :, KF * token : KF * (token + TILES)].rearrange(
                 "p h (j d) -> p h j d", j=TILES

@@ -56,6 +56,14 @@ def tile_multilatentattention_pb_t_kernel(
         wb_words = const.tile([P, KVR * PACK], U8, align_bytes=256)
         wb_scales = const.tile([P, KVR], U8, align_bytes=64)
 
+        zeros = const.tile([P, KVR], BF16)
+        nc.vector.memset(zeros[:], 0.0)
+
+        def keep_busy(products):
+            unread = psum.tile([P, KVR], F32, name="kv_tile0")
+            for i in range(products):
+                nc.tensor.matmul(unread[:], zeros[:, 0:P], zeros[:], start=True, stop=True)
+
         zero = const.tile([P, 1], F32)
         nc.vector.memset(zero[:], 0.0)
         sin_of_zero = const.tile([P, 1], F32)
@@ -303,10 +311,13 @@ def tile_multilatentattention_pb_t_kernel(
             run(expand, r - 2)
 
         permute_scales()
+        keep_busy(4)
         flip_x(0)
+        keep_busy(2)
         quantise_x(0)
         permute_words()
         flip_x(1)
+        keep_busy(2)
         quantise_x(1)
         sin_half = const.tile([P, TABLE], F32)
         nc.scalar.activation(out=sin_half[:], in_=part_turn[:], func=ACT.Sin, scale=math.pi)

import math

import concourse.mybir as mybir
from concourse.masks import make_identity

F32 = mybir.dt.float32
BF16 = mybir.dt.bfloat16
I32 = mybir.dt.int32
U32 = mybir.dt.uint32
U8 = mybir.dt.uint8
FP8X4 = mybir.dt.float8_e4m3fn_x4
ALU = mybir.AluOpType
ACT = mybir.ActivationFunctionType

P = 128
PACK = 4
B, N, E, H = 4, 1024, 1024, 4
NOPE, VDIM, ROPE, KVR = 64, 64, 128, 512
KF = NOPE + ROPE
PAIRS = ROPE // 2
X_PASSES = E // (P * PACK)
CKV = KVR + ROPE
TILES = 2
STEP = P * TILES
STEPS = B * N // STEP
STEPS_PER_BATCH = N // STEP
GROUP = 2
GROUPS = STEPS // GROUP
GROUPS_PER_BATCH = STEPS_PER_BATCH // GROUP
SINGLE_GROUPS = 4
ROWS = GROUP * TILES
BASE = 10000.0

FLOPS = 2 * B * N * (E * CKV + KVR * H * (NOPE + VDIM))

ROUND_MAGIC = 1.5 * 2.0**23


def tile_multilatentattention_pb_t_kernel(
    tc, x, Wkva_words, Wkva_scales, Wkvb_words, Wkvb_scales, kf, v
):
    nc = tc.nc
    with (
        tc.tile_pool(name="const", bufs=1) as const,
        tc.tile_pool(name="work", bufs=2) as work,
        tc.tile_pool(name="result", bufs=4) as result,
        tc.psum_pool(name="psum", bufs=1) as psum,
        tc.manual_schedule(),
    ):
        x_all = const.tile([P, STEPS, TILES, E], BF16, align_bytes=256)
        x_rows = x.flatten_outer_dims().rearrange("(q p a j) e -> p q a j e", p=P, a=GROUP, j=TILES)
        wa_words = const.tile([P, X_PASSES, CKV * PACK], U8, align_bytes=256)
        wa_scales = const.tile([P, X_PASSES, CKV], U8, align_bytes=64)
        wc_words = const.tile([P, X_PASSES, PACK, P * PACK], U8, align_bytes=64)
        wc_scales = const.tile([P, X_PASSES, PACK, P], U8, align_bytes=64)
        wb_words = const.tile([P, KVR * PACK], U8, align_bytes=256)
        wb_scales = const.tile([P, KVR], U8, align_bytes=64)

        zeros = const.tile([P, KVR], BF16)
        nc.vector.memset(zeros[:], 0.0)

        def keep_busy(products):
            unread = psum.tile([P, KVR], F32, name="kv_tile0")
            for i in range(products):
                nc.tensor.matmul(unread[:], zeros[:, 0:P], zeros[:], start=True, stop=True)

        zero = const.tile([P, 1], F32)
        nc.vector.memset(zero[:], 0.0)
        sin_of_zero = const.tile([P, 1], F32)
        nc.scalar.activation(out=sin_of_zero[:], in_=zero[:], func=ACT.Sin)

        nc.vector.memset(wa_scales[:].rearrange("p g n -> p (g n)").bitcast(I32), 0)
        nc.vector.memset(wb_scales[:].bitcast(I32), 0)

        def load_x(s):
            nc.sync.dma_start(out=x_all[:, s], in_=x_rows[:, s // GROUP, s % GROUP])

        def load_x_tile(s, j):
            nc.sync.dma_start(out=x_all[:, s, j], in_=x_rows[:, s // GROUP, s % GROUP, j])

        def load_wkva(first, last):
            nc.sync.dma_start(
                out=wa_words[:, :, PACK * first : PACK * last].bitcast(I32),
                in_=Wkva_words[:, :, first:last, :].rearrange("g p n t -> p g (n t)").bitcast(I32),
            )

        load_x_tile(0, 0)
        load_x_tile(0, 1)
        for quad in range(4):
            nc.sync.dma_start(
                out=wa_scales[32 * quad : 32 * quad + 4].bitcast(I32),
                in_=Wkva_scales[:, 4 * quad : 4 * quad + 4, :].rearrange("g r n -> r g n").bitcast(I32),
            )
        load_x(1)
        load_wkva(0, KVR)
        load_wkva(KVR, CKV)
        for quad in range(4):
            nc.sync.dma_start(
                out=wb_scales[32 * quad : 32 * quad + 4].bitcast(I32),
                in_=Wkvb_scales[0, 4 * quad : 4 * quad + 4, :].bitcast(I32),
            )
        nc.sync.dma_start(
            out=wb_words[:].bitcast(I32),
            in_=Wkvb_words[0].rearrange("p n t -> p (n t)").bitcast(I32),
        )
        for s in range(2, STEPS):
            load_x(s)

        x_grouped, x_codes, x_scales, pe_sums = {}, {}, {}, {}
        c_grouped, c_codes, c_scales, kv_sums, kf_rows = {}, {}, {}, {}, {}
        with_cos, with_sin, rows = {}, {}, {}

        def flip_x(s):
            x_grouped[s] = work.tile([P, TILES, X_PASSES, P, PACK], BF16, name="x_grouped", align_bytes=64)
            for j in range(TILES):
                flipped = psum.tile([P, X_PASSES, 2, P], F32, name="x_flipped", bufs=2)
                for g in range(X_PASSES):
                    for u in range(2):
                        words = x_all[:, s, j].bitcast(F32)[:, 2 * P * g + u : 2 * P * (g + 1) : 2]
                        nc.tensor.transpose(flipped[:, g, u, :], words, identity[:])
                nc.scalar.copy(
                    out=x_grouped[s][:, j].bitcast(F32), in_=flipped[:].rearrange("p g u t -> p g t u")
                )

        def quantise_x(s):
            x_codes[s] = work.tile([P, TILES, X_PASSES, P], U32, name="x_codes", align_bytes=64)
            x_scales[s] = work.tile([P, TILES, X_PASSES, P], U8, name="x_scales", align_bytes=64)
            for tiles in [slice(j, j + 1) for j in range(TILES)] if s == 0 else [slice(0, TILES)]:
                nc.vector.quantize_mx(
                    out=x_codes[s][:, tiles].rearrange("p j g t -> p (j g t)").bitcast(FP8X4),
                    scales=x_scales[s][:, tiles].rearrange("p j g t -> p (j g t)"),
                    in_=x_grouped[s][:, tiles].rearrange("p j g t k -> p (j g t k)"),
                )

        def x_times_wkva(s, j, first, width, sums):
            for g in range(X_PASSES):
                nc.tensor.matmul_mx(
                    out=sums,
                    lhsT=x_codes[s][:, j, g, :].bitcast(FP8X4),
                    lhsT_scale=x_scales[s][:, j, g, :],
                    rhs=wa_words[:, g, PACK * first : PACK * (first + width)].bitcast(FP8X4),
                    rhs_scale=wa_scales[:, g, first : first + width],
                    start=(g == 0),
                    stop=(g == X_PASSES - 1),
                )

        def permute_scales():
            nc.vector.tensor_copy(
                out=wc_scales[:], in_=wa_scales[:, :, 0:KVR].rearrange("p g (m t) -> p g t m", t=PACK)
            )

        def permute_words():
            nc.vector.tensor_copy(
                out=wc_words[:].bitcast(I32),
                in_=wa_words[:, :, 0 : KVR * PACK].bitcast(I32).rearrange("p g (m t) -> p g t m", t=PACK),
            )

        def compress(s):
            c_grouped[s] = work.tile([P, TILES, P, PACK], BF16, name="c_grouped", align_bytes=64)
            for j in range(TILES):
                c_flipped = psum.tile([P, PACK, P], F32, name="c_flipped", bufs=2)
                for t in range(PACK):
                    for g in range(X_PASSES):
                        nc.tensor.matmul_mx(
                            out=c_flipped[:, t, :],
                            lhsT=wc_words[:, g, t, :].bitcast(FP8X4),
                            lhsT_scale=wc_scales[:, g, t, :],
                            rhs=x_codes[s][:, j, g, :].bitcast(FP8X4),
                            rhs_scale=x_scales[s][:, j, g, :],
                            start=(g == 0),
                            stop=(g == X_PASSES - 1),
                        )
                nc.scalar.copy(out=c_grouped[s][:, j], in_=c_flipped[:].rearrange("p t n -> p n t"))
            pe_sums[s] = psum.tile([P, 2 * TILES, ROPE], F32, name="pe_sums", bufs=2)
            for j in range(TILES):
                x_times_wkva(s, j, KVR, ROPE, pe_sums[s][:, j, :])

        def quantise_c(s):
            c_codes[s] = work.tile([P, TILES, P], U32, name="c_codes", align_bytes=64)
            c_scales[s] = work.tile([P, TILES, P], U8, name="c_scales", align_bytes=64)
            nc.vector.quantize_mx(
                out=c_codes[s][:].rearrange("p j t -> p (j t)").bitcast(FP8X4),
                scales=c_scales[s][:].rearrange("p j t -> p (j t)"),
                in_=c_grouped[s][:].rearrange("p j t k -> p (j t k)"),
            )

        def rotation_products(s):
            pe = pe_sums[s][:, 0:TILES].rearrange("p j (i e) -> p j e i", e=2)
            cos = cos_table[:, s % STEPS_PER_BATCH]
            sin = sin_table[:, s % STEPS_PER_BATCH]
            with_cos[s] = work.tile([P, TILES, 2, PAIRS], F32, name="with_cos")
            with_sin[s] = work.tile([P, TILES, 2, PAIRS], F32, name="with_sin")
            nc.vector.tensor_tensor(
                out=with_cos[s][:], in0=pe, in1=cos.unsqueeze(2).to_broadcast([P, TILES, 2, PAIRS]), op=ALU.mult
            )
            nc.vector.tensor_tensor(out=with_sin[s][:], in0=pe[:, :, ::-1, :], in1=sin, op=ALU.mult)

        def stored_together(s):
            if s // GROUP < GROUPS - SINGLE_GROUPS:
                return GROUP * (s // GROUP), GROUP
            return s, 1

        def rotation_sum(s):
            first_step, steps = stored_together(s)
            if s == first_step:
                rows[first_step] = result.tile(
                    [P, H, steps * TILES * (KF + VDIM)], F32, name="rows", align_bytes=256
                )
            token = TILES * (s - first_step)
            kf_rows[s] = rows[first_step][:, :, KF * token : KF * (token + TILES)].rearrange(
                "p h (j d) -> p h j d", j=TILES
            )
            nc.vector.tensor_tensor(
                out=kf_rows[s][:, 0, :, NOPE:KF].rearrange("p j (i e) -> p j i e", e=2),
                in0=with_cos[s][:].rearrange("p j e i -> p j i e"),
                in1=with_sin[s][:].rearrange("p j e i -> p j i e"),
                op=ALU.add,
            )

        def repeat_for_heads(s):
            nc.vector.tensor_copy(
                out=kf_rows[s][:, 1:H, :, NOPE:KF],
                in_=kf_rows[s][:, 0:1, :, NOPE:KF].to_broadcast([P, H - 1, TILES, ROPE]),
            )

        def c_times_wkvb(s, j, first, width, sums):
            nc.tensor.matmul_mx(
                out=sums,
                lhsT=c_codes[s][:, j, :].bitcast(FP8X4),
                lhsT_scale=c_scales[s][:, j, :],
                rhs=wb_words[:, PACK * first : PACK * (first + width)].bitcast(FP8X4),
                rhs_scale=wb_scales[:, first : first + width],
                start=True,
                stop=True,
            )

        def expand(s):
            kv_sums[s, 0] = psum.tile([P, KVR], F32, name="kv_tile0")
            kv_sums[s, 1] = psum.tile([P, KVR], F32, name="kv_tile1")
            c_times_wkvb(s, 0, 0, KVR, kv_sums[s, 0][:])
            c_times_wkvb(s, 1, 0, KVR, kv_sums[s, 1][:])

        def store(s):
            first_step, steps = stored_together(s)
            n = steps * TILES
            units = rows[first_step][:].rearrange("p h (u d) -> p h u d", d=NOPE)
            m = TILES * (s - first_step)
            tile0 = units[:, :, 3 * m : 3 * n + m + 1 : 3 * n - 2 * m, :]
            tile1 = units[:, :, 3 * (m + 1) : 3 * n + m + 2 : 3 * n - 2 * (m + 1), :]
            copy_tile1 = nc.scalar.copy if s >= STEPS - 3 else nc.vector.tensor_copy
            nc.scalar.copy(out=tile0, in_=kv_sums[s, 0][:].rearrange("p (h c d) -> p h c d", c=2, d=NOPE))
            copy_tile1(out=tile1, in_=kv_sums[s, 1][:].rearrange("p (h c d) -> p h c d", c=2, d=NOPE))
            if s == first_step + steps - 1:
                q = s // GROUP
                b, first = q // GROUPS_PER_BATCH, GROUP * STEP * (q % GROUPS_PER_BATCH)
                skipped = TILES * (first_step % GROUP)
                for out, start, width in ((kf, 0, KF), (v, n * KF, VDIM)):
                    nc.sync.dma_start(
                        out=out[b, :, first : first + GROUP * STEP, :].rearrange("h (p t) d -> p h (t d)", t=ROWS)[
                            :, :, width * skipped : width * (skipped + n)
                        ],
                        in_=rows[first_step][:, :, start : start + n * width],
                    )

        TABLE = STEPS_PER_BATCH * TILES * PAIRS
        position_int = const.tile([P, STEPS_PER_BATCH * TILES], I32)
        nc.gpsimd.iota(
            position_int[:], pattern=[[GROUP * STEP, GROUPS_PER_BATCH], [1, ROWS]], base=0, channel_multiplier=ROWS
        )
        identity = const.tile([P, P], F32)
        make_identity(nc, identity[:])

        ratio = BASE ** (-2.0 / ROPE)
        turns = const.tile([P, STEPS_PER_BATCH * TILES, PAIRS], F32)
        width = 8
        for i in range(width):
            nc.vector.tensor_scalar_mul(turns[:, :, i], position_int[:], ratio**i * 0.5 / math.pi)
        while width < PAIRS:
            nc.vector.tensor_scalar_mul(turns[:, :, width : 2 * width], turns[:, :, 0:width], ratio**width)
            width *= 2
        whole_turns = const.tile([P, TABLE], F32)
        nc.vector.tensor_scalar(
            out=whole_turns[:],
            in0=turns[:].rearrange("p n i -> p (n i)"),
            scalar1=ROUND_MAGIC,
            scalar2=-ROUND_MAGIC,
            op0=ALU.add,
            op1=ALU.add,
        )
        part_turn = const.tile([P, TABLE], F32)
        nc.vector.tensor_tensor(
            out=part_turn[:], in0=turns[:].rearrange("p n i -> p (n i)"), in1=whole_turns[:], op=ALU.subtract
        )
        def run(stage, s):
            if 0 <= s < STEPS:
                stage(s)

        def pipeline_round(r):
            if r >= STEPS:
                run(quantise_c, r - 2)
            run(store, r - 3)
            run(rotation_products, r - 2)
            if r < STEPS:
                run(quantise_c, r - 2)
            run(rotation_sum, r - 2)
            if r > 1:
                run(flip_x, r)
                run(quantise_x, r)
            run(repeat_for_heads, r - 2)
            run(compress, r - 1)
            run(expand, r - 2)

        permute_scales()
        keep_busy(4)
        flip_x(0)
        keep_busy(2)
        quantise_x(0)
        permute_words()
        flip_x(1)
        keep_busy(2)
        quantise_x(1)
        sin_half = const.tile([P, TABLE], F32)
        nc.scalar.activation(out=sin_half[:], in_=part_turn[:], func=ACT.Sin, scale=math.pi)
        sin_table = const.tile([P, STEPS_PER_BATCH, TILES, 2, PAIRS], F32)
        for e, sign in ((0, -1.0), (1, 1.0)):
            nc.scalar.activation(
                out=sin_table[:, :, :, e, :].rearrange("p r j i -> p (r j) i"),
                in_=part_turn[:].rearrange("p (n i) -> p n i", i=PAIRS),
                func=ACT.Sin,
                scale=sign * 2.0 * math.pi,
            )
        minus_two_squares = const.tile([P, TABLE], F32)
        nc.vector.scalar_tensor_tensor(
            out=minus_two_squares[:], in0=sin_half[:], scalar=-2.0, in1=sin_half[:], op0=ALU.mult, op1=ALU.mult
        )
        cos_table = const.tile([P, STEPS_PER_BATCH, TILES, PAIRS], F32)
        nc.vector.tensor_scalar_add(cos_table[:].rearrange("p r j i -> p (r j i)"), minus_two_squares[:], 1.0)
        for r in range(1, STEPS + 3):
            pipeline_round(r)
